import numpy as np
import ml_dtypes


def mxq(x, axis, fmt="e4m3"):
    dtype, down = {"e4m3": (ml_dtypes.float8_e4m3fn, 7), "e5m2": (ml_dtypes.float8_e5m2, 14)}[fmt]
    v = np.moveaxis(np.asarray(x, np.float32).astype(ml_dtypes.bfloat16).astype(np.float64), axis, -1)
    blocks = v.reshape(v.shape[:-1] + (-1, 32))
    amax = np.abs(blocks).max(-1, keepdims=True)
    byte = np.maximum(np.where(amax > 0, np.frexp(amax)[1] - 1 + 127, 0) - down, 1)
    scale = np.exp2(byte - 127.0)
    codes = (blocks / scale).astype(np.float32).astype(dtype).astype(np.float64)
    return np.moveaxis((codes * scale).reshape(v.shape), -1, axis)


WIDE = False


def mx_kscale(k):
    if not WIDE:
        return np.ones(k)
    levels = np.array([10, -10, 5, -5, 0])
    a = np.random.permutation(np.resize(levels, k // 512 * 4)).reshape(k // 512, 4)
    idx = np.arange(k)
    return np.exp2(a[idx // 512, idx % 128 // 32])


BF16 = ml_dtypes.bfloat16


def bf(x):
    return np.asarray(x, np.float32).astype(BF16)


def f64(x):
    return np.asarray(x).astype(np.float64)


N, C, D, HD, O = 1024, 128, 8192, 1024, 512
NPC = N // C


def silu(v):
    return v / (1.0 + np.exp(-v))


def row_norm(V):
    return np.sqrt((V * V).sum(axis=1))


def wn_weight(V, g):
    return V * (g / row_norm(V))[:, None]


def setup_inputs():
    s = mx_kscale(D)
    count = np.random.randint(0, 2 * NPC + 1, (C, 1))
    pooled_sum = np.random.standard_normal((C, D)) * 2.0 * np.sqrt(np.maximum(count, 1))
    V0 = np.random.standard_normal((HD, D)) * (0.5 + np.random.random((HD, 1))) / np.sqrt(D)
    g0 = 2.0 * (1.0 + 0.1 * np.random.standard_normal(HD))
    g0 = g0 * row_norm(V0 / s) / row_norm(V0)
    V1 = np.random.standard_normal((HD, HD)) * (0.5 + np.random.random((HD, 1))) / np.sqrt(HD)
    g1 = 2.0 * (1.0 + 0.1 * np.random.standard_normal(HD))
    return {"pooled_sum": bf(pooled_sum * s), "count": bf(count),
            "V0": bf(V0 / s), "g0": bf(g0), "b0": bf(np.random.standard_normal(HD) * 0.2),
            "V1": bf(V1), "g1": bf(g1), "b1": bf(np.random.standard_normal(HD) * 0.2)}


def reference(pooled_sum, count, V0, g0, b0, V1, g1, b1):
    h = f64(pooled_sum) / np.maximum(f64(count), 1.0)
    W0 = wn_weight(f64(V0), f64(g0))
    a0 = silu((mxq(h, 1, "e4m3") @ mxq(W0, 1, "e4m3").T) + f64(b0))
    W1 = wn_weight(f64(V1), f64(g1))
    return silu((mxq(a0, 1, "e4m3") @ mxq(W1, 1, "e4m3").T) + f64(b1))

@@ -1,0 +1,227 @@
+from contextlib import ExitStack
+
+import concourse.mybir as mybir
+from concourse.masks import make_identity
+
+BF16 = mybir.dt.bfloat16
+F32 = mybir.dt.float32
+U32 = mybir.dt.uint32
+U8 = mybir.dt.uint8
+FP8X4 = mybir.dt.float8_e4m3fn_x4
+ALU = mybir.AluOpType
+ACT = mybir.ActivationFunctionType
+
+P = 128
+D_IN = 8192
+HIDDEN = 1024
+K_PASS = 512
+
+SLAB = 8192
+SLAB_PASSES = SLAB // K_PASS
+HALF = SLAB // 2
+HALF_PASSES = SLAB_PASSES // 2
+BANK_PASSES = 2
+HALF_BANKS = HALF_PASSES // BANK_PASSES
+V0_SLABS = HIDDEN // P
+V1_ROWS = SLAB // HIDDEN
+SCALAR_EVERY = 8
+
+FLOPS = 2 * P * D_IN * HIDDEN + 2 * P * HIDDEN * HIDDEN
+
+
+def tile_hypernetfullyconnectedflexilayersizearch_pa_k_kernel(
+    tc, pooled_sum, count, V0, g0, b0, V1, g1, b1, out
+):
+    nc = tc.nc
+    with ExitStack() as ctx:
+        const = ctx.enter_context(tc.tile_pool(name="const", bufs=1))
+        slabs = ctx.enter_context(tc.tile_pool(name="slabs", bufs=5))
+        scratch = ctx.enter_context(tc.tile_pool(name="scratch", bufs=2))
+        stats = ctx.enter_context(tc.tile_pool(name="stats", bufs=4))
+        regroup = ctx.enter_context(tc.tile_pool(name="regroup", bufs=3))
+        weights = ctx.enter_context(tc.tile_pool(name="weights", bufs=2))
+        final = ctx.enter_context(tc.tile_pool(name="final", bufs=2))
+        psum_t = ctx.enter_context(tc.psum_pool(name="psum_t", bufs=6))
+        psum_acc = ctx.enter_context(tc.psum_pool(name="psum_acc", bufs=2))
+
+        ident = const.tile([P, P], F32)
+        make_identity(nc, ident[:])
+        minus_half = const.tile([P, V1_ROWS], F32)
+        nc.vector.memset(minus_half[:], -0.5)
+
+        vec_rows = const.tile([P, P], F32)
+        nc.vector.memset(vec_rows[:], 0.0)
+        vec_rows_bf = vec_rows[:].bitcast(BF16)
+        for n, vec in enumerate((g0, b0, g1)):
+            nc.sync.dma_start(
+                out=vec_rows_bf[4 * n : 4 * n + 4, :],
+                in_=vec.rearrange("(r w) -> r w", r=4),
+            )
+        cnt = const.tile([P, 1], BF16)
+        nc.sync.dma_start(out=cnt[:], in_=count)
+
+        vec_t = psum_t.tile([P, P], F32, tag="xt")
+        nc.tensor.transpose(vec_t[:], vec_rows[:], ident[:])
+        vecs = const.tile([P, 3 * V0_SLABS], F32)
+        nc.vector.tensor_copy(out=vecs[:], in_=vec_t[:, 0:12].bitcast(BF16))
+        gain0 = vecs[:, 0:V0_SLABS]
+        bias0 = vecs[:, V0_SLABS : 2 * V0_SLABS]
+        gain1 = vecs[:, 2 * V0_SLABS : 3 * V0_SLABS]
+
+        per_count = const.tile([P, 1], F32)
+        nc.vector.tensor_scalar_max(out=per_count[:], in0=cnt[:], scalar1=1.0)
+        nc.vector.reciprocal(out=per_count[:], in_=per_count[:])
+
+        def sum_of_squares(values, total):
+            squares = scratch.tile([P, HALF], BF16)
+            width = values.shape[1]
+            nc.scalar.activation(
+                out=squares[:, 0:width], in_=values, func=ACT.Square, accum_out=total
+            )
+
+        def quantise_half(slab, half, codes, scales):
+            words = slab[:].bitcast(F32)
+            grouped = regroup.tile([P, HALF_PASSES, P, 2], F32, align_bytes=64)
+            for bank in range(HALF_BANKS):
+                first_block = 2 * BANK_PASSES * (HALF_BANKS * half + bank)
+                xt = psum_t.tile([P, 2 * BANK_PASSES, P], F32)
+                for i in range(2 * BANK_PASSES):
+                    block = first_block + i
+                    nc.tensor.transpose(
+                        xt[:, i, :], words[:, block * P : (block + 1) * P], ident[:]
+                    )
+                passes = slice(BANK_PASSES * bank, BANK_PASSES * (bank + 1))
+                planes = xt[:].rearrange("p (g u) r -> p g r u", u=2)
+                if (HALF_BANKS * half + bank) % SCALAR_EVERY == 0:
+                    nc.scalar.copy(out=grouped[:, passes, :, :], in_=planes)
+                else:
+                    nc.vector.tensor_copy(out=grouped[:, passes, :, :], in_=planes)
+            passes = slice(HALF_PASSES * half, HALF_PASSES * (half + 1))
+            nc.vector.quantize_mx(
+                out=codes[:, passes, :].rearrange("p n r -> p (n r)").bitcast(FP8X4),
+                scales=scales[:, passes, :].rearrange("p n r -> p (n r)"),
+                in_=grouped[:].rearrange("p n r u -> p (n r u)").bitcast(BF16),
+            )
+
+        halves = [slice(0, HALF), slice(HALF, SLAB)]
+        v0_rows = V0.rearrange("(i2 p e) k -> i2 e p k", p=P, e=2)
+
+        def load_half(slab, rows, half):
+            nc.sync.dma_start(out=slab[:, halves[half]], in_=rows[:, halves[half]])
+
+        first_slab = slabs.tile([P, SLAB], BF16, tag="slab")
+        h_slab = slabs.tile([P, SLAB], BF16, tag="slab")
+        for half in range(2):
+            load_half(first_slab, v0_rows[0, 0], half)
+            load_half(h_slab, pooled_sum, half)
+
+        h_codes = const.tile([P, SLAB_PASSES, P], U32, align_bytes=64)
+        h_scales = const.tile([P, SLAB_PASSES, P], U8, align_bytes=64)
+        for half in range(2):
+            nc.vector.tensor_scalar_mul(
+                out=h_slab[:, halves[half]], in0=h_slab[:, halves[half]], scalar1=per_count[:]
+            )
+            quantise_half(h_slab, half, h_codes, h_scales)
+
+        a0_grouped = const.tile([P, HIDDEN // K_PASS, P, 4], BF16, align_bytes=64)
+        for i in range(V0_SLABS):
+            slab = first_slab if i == 0 else slabs.tile([P, SLAB], BF16, tag="slab", name="slab")
+            sums = stats.tile([P, 2], F32)
+            for half in range(2):
+                if i > 0:
+                    load_half(slab, v0_rows[i // 2, i % 2], half)
+                sum_of_squares(slab[:, halves[half]], sums[:, half : half + 1])
+            row_scale = stats.tile([P, 1], F32)
+            nc.gpsimd.tensor_tensor(
+                out=row_scale[:], in0=sums[:, 0:1], in1=sums[:, 1:2], op=ALU.add
+            )
+            nc.gpsimd.tensor_tensor(
+                out=row_scale[:], in0=row_scale[:], in1=minus_half[:, 0:1], op=ALU.pow
+            )
+            nc.gpsimd.tensor_tensor(
+                out=row_scale[:], in0=row_scale[:], in1=gain0[:, i : i + 1], op=ALU.mult
+            )
+            w_codes = weights.tile([P, SLAB_PASSES, P], U32, align_bytes=64)
+            w_scales = weights.tile([P, SLAB_PASSES, P], U8, align_bytes=64)
+            for half in range(2):
+                nc.vector.tensor_scalar_mul(
+                    out=slab[:, halves[half]], in0=slab[:, halves[half]], scalar1=row_scale[:]
+                )
+                quantise_half(slab, half, w_codes, w_scales)
+            acc = psum_acc.tile([P, P], F32, tag="acc")
+            for n in range(SLAB_PASSES):
+                nc.tensor.matmul_mx(
+                    out=acc[:],
+                    lhsT=w_codes[:, n, :].bitcast(FP8X4),
+                    lhsT_scale=w_scales[:, n, :],
+                    rhs=h_codes[:, n, :].bitcast(FP8X4),
+                    rhs_scale=h_scales[:, n, :],
+                    start=(n == 0),
+                    stop=(n == SLAB_PASSES - 1),
+                )
+            nc.scalar.activation(
+                out=a0_grouped[:, i // 4, :, i % 4],
+                in_=acc[:],
+                func=ACT.Silu,
+                bias=bias0[:, i : i + 1],
+            )
+
+        a0_codes = const.tile([P, HIDDEN // K_PASS, P], U32, align_bytes=64)
+        a0_scales = const.tile([P, HIDDEN // K_PASS, P], U8, align_bytes=64)
+        nc.vector.quantize_mx(
+            out=a0_codes[:].rearrange("p n c -> p (n c)").bitcast(FP8X4),
+            scales=a0_scales[:].rearrange("p n c -> p (n c)"),
+            in_=a0_grouped[:].rearrange("p n c t -> p (n c t)"),
+        )
+
+        v1_rows = V1.rearrange("(i2 p e) k -> p i2 (e k)", p=P, e=2)
+        w1_slab = slabs.tile([P, SLAB], BF16, tag="slab")
+        w1_sums = stats.tile([P, V1_ROWS], F32)
+        for half in range(2):
+            nc.sync.dma_start(
+                out=w1_slab[:, halves[half]].rearrange("p (i2 w) -> p i2 w", i2=2),
+                in_=v1_rows[:, 2 * half : 2 * half + 2, :],
+            )
+        b1_all = const.tile([P, HIDDEN], BF16)
+        nc.sync.dma_start(out=b1_all[:], in_=b1.partition_broadcast(P))
+        for i in range(V1_ROWS):
+            sum_of_squares(w1_slab[:, i * HIDDEN : (i + 1) * HIDDEN], w1_sums[:, i : i + 1])
+        w1_scale = stats.tile([P, V1_ROWS], F32)
+        nc.gpsimd.tensor_tensor(out=w1_scale[:], in0=w1_sums[:], in1=minus_half[:], op=ALU.pow)
+        nc.gpsimd.tensor_tensor(out=w1_scale[:], in0=w1_scale[:], in1=gain1, op=ALU.mult)
+        w1_codes = const.tile([P, SLAB_PASSES, P], U32, align_bytes=64)
+        w1_scales = const.tile([P, SLAB_PASSES, P], U8, align_bytes=64)
+        for half in range(2):
+            for i in range(half * V1_ROWS // 2, (half + 1) * V1_ROWS // 2):
+                row = slice(i * HIDDEN, (i + 1) * HIDDEN)
+                nc.vector.tensor_scalar_mul(
+                    out=w1_slab[:, row], in0=w1_slab[:, row], scalar1=w1_scale[:, i : i + 1]
+                )
+            quantise_half(w1_slab, half, w1_codes, w1_scales)
+
+        passes = HIDDEN // K_PASS
+        for bank in range(2):
+            cols = slice(bank * 512, (bank + 1) * 512)
+            acc = psum_acc.tile([P, 512], F32, tag="acc")
+            for q in range(4):
+                i = 4 * bank + q
+                for n in range(passes):
+                    nc.tensor.matmul_mx(
+                        out=acc[:, q * P : (q + 1) * P],
+                        lhsT=a0_codes[:, n, :].bitcast(FP8X4),
+                        lhsT_scale=a0_scales[:, n, :],
+                        rhs=w1_codes[:, passes * i + n, :].bitcast(FP8X4),
+                        rhs_scale=w1_scales[:, passes * i + n, :],
+                        start=(n == 0),
+                        stop=(n == passes - 1),
+                    )
+            biased = final.tile([P, 512], F32)
+            nc.vector.tensor_tensor(
+                out=biased[:].rearrange("c (i2 p e) -> c i2 p e", i2=2, e=2),
+                in0=acc[:].rearrange("c (i2 e p) -> c i2 p e", i2=2, e=2),
+                in1=b1_all[:, cols].rearrange("c (i2 p e) -> c i2 p e", i2=2, e=2),
+                op=ALU.add,
+            )
+            result = final.tile([P, 512], F32)
+            nc.scalar.activation(out=result[:], in_=biased[:], func=ACT.Silu)
+            nc.sync.dma_start(out=out[:, cols], in_=result[:])

@@ -15,16 +15,23 @@ P = 128
 D_IN = 8192
 HIDDEN = 1024
 K_PASS = 512
+BANK = 512
 
 SLAB = 8192
-SLAB_PASSES = SLAB // K_PASS
 HALF = SLAB // 2
+SLAB_PASSES = SLAB // K_PASS
 HALF_PASSES = SLAB_PASSES // 2
-BANK_PASSES = 2
-HALF_BANKS = HALF_PASSES // BANK_PASSES
+HALF_BANKS = HALF // 2 // BANK
+BANK_BLOCKS = BANK // P
+H_SLAB = 0
 V0_SLABS = HIDDEN // P
+V1_SLAB = V0_SLABS + 1
+SLABS = V1_SLAB + 1
+UNITS = 2 * SLABS
 V1_ROWS = SLAB // HIDDEN
-SCALAR_EVERY = 8
+L1_PASSES = HIDDEN // K_PASS
+LEAD = 2
+SCALAR_UNITS = 3
 
 FLOPS = 2 * P * D_IN * HIDDEN + 2 * P * HIDDEN * HIDDEN
 
@@ -43,185 +50,235 @@ def tile_hypernetfullyconnectedflexilayersizearch_pa_k_kernel(
         final = ctx.enter_context(tc.tile_pool(name="final", bufs=2))
         psum_t = ctx.enter_context(tc.psum_pool(name="psum_t", bufs=6))
         psum_acc = ctx.enter_context(tc.psum_pool(name="psum_acc", bufs=2))
+        ctx.enter_context(tc.manual_schedule())
+        v0_rows = V0.rearrange("(i2 p e) (a w) -> i2 e p a w", p=P, e=2, a=4)
+        dram_rows = {H_SLAB: pooled_sum.rearrange("c (a w) -> c a w", a=4)}
+        for i in range(V0_SLABS):
+            dram_rows[1 + i] = v0_rows[i // 2, i % 2]
+        dram_rows[V1_SLAB] = V1.rearrange("(a p e) k -> p a (e k)", p=P, e=2)
+
+        slab_tile = {}
+        factor = {}
+        codes = {}
+        planes = {}
+        banks = {}
+        grouped = {}
+        product = {}
+
+        def new_slab(s):
+            slab_tile[s] = slabs.tile([P, SLAB], BF16, name="slab")
+
+        def fetch_half(s, x):
+            nc.sync.dma_start(
+                out=slab_tile[s][:, x * HALF : (x + 1) * HALF].rearrange(
+                    "p (a w) -> p a w", a=2
+                ),
+                in_=dram_rows[s][:, 2 * x : 2 * x + 2, :],
+            )
+
+        cnt = const.tile([P, 1], BF16)
+        nc.sync.dma_start(out=cnt[:], in_=count)
+        vec_rows = const.tile([P, P], F32)
+        nc.vector.memset(vec_rows[:], 0.0)
+        for n, vec in enumerate((g0, b0, g1)):
+            nc.sync.dma_start(
+                out=vec_rows[:].bitcast(BF16)[4 * n : 4 * n + 4, :],
+                in_=vec.rearrange("(r w) -> r w", r=4),
+            )
+
+        new_slab(1)
+        new_slab(H_SLAB)
+        for x in range(2):
+            fetch_half(1, x)
+            fetch_half(H_SLAB, x)
 
         ident = const.tile([P, P], F32)
         make_identity(nc, ident[:])
         minus_half = const.tile([P, V1_ROWS], F32)
         nc.vector.memset(minus_half[:], -0.5)
 
-        vec_rows = const.tile([P, P], F32)
-        nc.vector.memset(vec_rows[:], 0.0)
-        vec_rows_bf = vec_rows[:].bitcast(BF16)
-        for n, vec in enumerate((g0, b0, g1)):
-            nc.sync.dma_start(
-                out=vec_rows_bf[4 * n : 4 * n + 4, :],
-                in_=vec.rearrange("(r w) -> r w", r=4),
-            )
-        cnt = const.tile([P, 1], BF16)
-        nc.sync.dma_start(out=cnt[:], in_=count)
-
         vec_t = psum_t.tile([P, P], F32, tag="xt")
         nc.tensor.transpose(vec_t[:], vec_rows[:], ident[:])
         vecs = const.tile([P, 3 * V0_SLABS], F32)
         nc.vector.tensor_copy(out=vecs[:], in_=vec_t[:, 0:12].bitcast(BF16))
-        gain0 = vecs[:, 0:V0_SLABS]
         bias0 = vecs[:, V0_SLABS : 2 * V0_SLABS]
-        gain1 = vecs[:, 2 * V0_SLABS : 3 * V0_SLABS]
+        gain = {V1_SLAB: vecs[:, 2 * V0_SLABS : 3 * V0_SLABS]}
+        for i in range(V0_SLABS):
+            gain[1 + i] = vecs[:, i : i + 1]
+        b1_all = const.tile([P, HIDDEN], BF16)
 
         per_count = const.tile([P, 1], F32)
         nc.vector.tensor_scalar_max(out=per_count[:], in0=cnt[:], scalar1=1.0)
         nc.vector.reciprocal(out=per_count[:], in_=per_count[:])
+        factor[H_SLAB] = per_count[:]
 
-        def sum_of_squares(values, total):
-            squares = scratch.tile([P, HALF], BF16)
-            width = values.shape[1]
-            nc.scalar.activation(
-                out=squares[:, 0:width], in_=values, func=ACT.Square, accum_out=total
-            )
+        def row_factors(s):
+            rows = gain[s].shape[1]
+            piece = min(SLAB // rows, HALF)
+            sums = stats.tile([P, SLAB // piece], F32, name="sums%d" % rows)
+            factor[s] = stats.tile([P, rows], F32, name="factor%d" % rows)[:]
+            for x in range(2):
+                for n in range(x * HALF // piece, (x + 1) * HALF // piece):
+                    squares = scratch.tile([P, HALF], BF16, name="squares")
+                    nc.scalar.activation(
+                        out=squares[:, 0:piece],
+                        in_=slab_tile[s][:, n * piece : (n + 1) * piece],
+                        func=ACT.Square,
+                        accum_out=sums[:, n : n + 1],
+                    )
+                if rows == 1 and x == 0:
+                    continue
+                if rows == 1:
+                    mine = factor[s]
+                    nc.gpsimd.tensor_tensor(
+                        out=mine, in0=sums[:, 0:1], in1=sums[:, 1:2], op=ALU.add
+                    )
+                    lengths, gains = mine, gain[s]
+                else:
+                    cols = slice(x * rows // 2, (x + 1) * rows // 2)
+                    mine, lengths, gains = factor[s][:, cols], sums[:, cols], gain[s][:, cols]
+                width = mine.shape[1]
+                nc.gpsimd.tensor_tensor(
+                    out=mine, in0=lengths, in1=minus_half[:, 0:width], op=ALU.pow
+                )
+                nc.gpsimd.tensor_tensor(out=mine, in0=mine, in1=gains, op=ALU.mult)
 
-        def quantise_half(slab, half, codes, scales):
-            words = slab[:].bitcast(F32)
-            grouped = regroup.tile([P, HALF_PASSES, P, 2], F32, align_bytes=64)
-            for bank in range(HALF_BANKS):
-                first_block = 2 * BANK_PASSES * (HALF_BANKS * half + bank)
-                xt = psum_t.tile([P, 2 * BANK_PASSES, P], F32)
-                for i in range(2 * BANK_PASSES):
-                    block = first_block + i
+        def prepare(s):
+            new_slab(s)
+            for x in range(2):
+                fetch_half(s, x)
+            if s == V1_SLAB:
+                nc.sync.dma_start(out=b1_all[:], in_=b1.partition_broadcast(P))
+            row_factors(s)
+
+        def scale(m):
+            s, x = divmod(m, 2)
+            span = SLAB // factor[s].shape[1]
+            piece = min(span, HALF)
+            for start in range(x * HALF, (x + 1) * HALF, piece):
+                values = slab_tile[s][:, start : start + piece]
+                nc.vector.tensor_scalar_mul(
+                    out=values,
+                    in0=values,
+                    scalar1=factor[s][:, start // span : start // span + 1],
+                )
+
+        def transposes(m):
+            s, x = divmod(m, 2)
+            words = slab_tile[s][:].bitcast(F32)
+            banks[m] = []
+            for b in range(HALF_BANKS):
+                xt = psum_t.tile([P, BANK_BLOCKS, P], F32, name="xt")
+                for i in range(BANK_BLOCKS):
+                    block = BANK_BLOCKS * (HALF_BANKS * x + b) + i
                     nc.tensor.transpose(
                         xt[:, i, :], words[:, block * P : (block + 1) * P], ident[:]
                     )
-                passes = slice(BANK_PASSES * bank, BANK_PASSES * (bank + 1))
-                planes = xt[:].rearrange("p (g u) r -> p g r u", u=2)
-                if (HALF_BANKS * half + bank) % SCALAR_EVERY == 0:
-                    nc.scalar.copy(out=grouped[:, passes, :, :], in_=planes)
+                banks[m].append(xt)
+
+        def empty_banks(m):
+            grouped[m] = regroup.tile([P, HALF_PASSES, P, 2], F32, name="grouped", align_bytes=64)
+            for b, xt in enumerate(banks[m]):
+                target = grouped[m][:, 2 * b : 2 * b + 2, :, :]
+                planes_uv = xt[:].rearrange("p (n u) r -> p n r u", u=2)
+                if m >= UNITS - SCALAR_UNITS:
+                    nc.scalar.copy(out=target, in_=planes_uv)
                 else:
-                    nc.vector.tensor_copy(out=grouped[:, passes, :, :], in_=planes)
-            passes = slice(HALF_PASSES * half, HALF_PASSES * (half + 1))
+                    nc.vector.tensor_copy(out=target, in_=planes_uv)
+
+        def quantise(m):
+            s, x = divmod(m, 2)
+            if x == 0:
+                pool = weights if 1 <= s <= V0_SLABS else const
+                label = "w0" if 1 <= s <= V0_SLABS else "slab%d" % s
+                codes[s] = pool.tile(
+                    [P, SLAB_PASSES, P], U32, name=label + "_codes", align_bytes=64
+                )
+                planes[s] = pool.tile(
+                    [P, SLAB_PASSES, P], U8, name=label + "_planes", align_bytes=64
+                )
+            passes = slice(HALF_PASSES * x, HALF_PASSES * (x + 1))
             nc.vector.quantize_mx(
-                out=codes[:, passes, :].rearrange("p n r -> p (n r)").bitcast(FP8X4),
-                scales=scales[:, passes, :].rearrange("p n r -> p (n r)"),
-                in_=grouped[:].rearrange("p n r u -> p (n r u)").bitcast(BF16),
+                out=codes[s][:, passes, :].rearrange("p n r -> p (n r)").bitcast(FP8X4),
+                scales=planes[s][:, passes, :].rearrange("p n r -> p (n r)"),
+                in_=grouped[m][:].rearrange("p n r u -> p (n r u)").bitcast(BF16),
             )
 
-        halves = [slice(0, HALF), slice(HALF, SLAB)]
-        v0_rows = V0.rearrange("(i2 p e) k -> i2 e p k", p=P, e=2)
+        a0_grouped = const.tile([P, L1_PASSES, P, 4], BF16, align_bytes=64)
+        a0_codes = const.tile([P, L1_PASSES, P], U32, align_bytes=64)
+        a0_planes = const.tile([P, L1_PASSES, P], U8, align_bytes=64)
 
-        def load_half(slab, rows, half):
-            nc.sync.dma_start(out=slab[:, halves[half]], in_=rows[:, halves[half]])
+        def multiply(m):
+            s, x = divmod(m, 2)
+            if 1 <= s <= V0_SLABS:
+                if x == 0:
+                    product[s] = psum_acc.tile([P, P], F32, name="acc")
+                for n in range(HALF_PASSES * x, HALF_PASSES * (x + 1)):
+                    nc.tensor.matmul_mx(
+                        out=product[s][:],
+                        lhsT=codes[s][:, n, :].bitcast(FP8X4),
+                        lhsT_scale=planes[s][:, n, :],
+                        rhs=codes[H_SLAB][:, n, :].bitcast(FP8X4),
+                        rhs_scale=planes[H_SLAB][:, n, :],
+                        start=(n == 0),
+                        stop=(n == SLAB_PASSES - 1),
+                    )
+            if s == V1_SLAB:
+                if x == 0:
+                    nc.vector.quantize_mx(
+                        out=a0_codes[:].rearrange("p n c -> p (n c)").bitcast(FP8X4),
+                        scales=a0_planes[:].rearrange("p n c -> p (n c)"),
+                        in_=a0_grouped[:].rearrange("p n c t -> p (n c t)"),
+                    )
+                product[m] = psum_t.tile([P, BANK], F32, tag="xt", name="out_bank")
+                for q in range(V1_ROWS // 2):
+                    i = x * V1_ROWS // 2 + q
+                    for n in range(L1_PASSES):
+                        nc.tensor.matmul_mx(
+                            out=product[m][:, q * P : (q + 1) * P],
+                            lhsT=a0_codes[:, n, :].bitcast(FP8X4),
+                            lhsT_scale=a0_planes[:, n, :],
+                            rhs=codes[s][:, L1_PASSES * i + n, :].bitcast(FP8X4),
+                            rhs_scale=planes[s][:, L1_PASSES * i + n, :],
+                            start=(n == 0),
+                            stop=(n == L1_PASSES - 1),
+                        )
 
-        first_slab = slabs.tile([P, SLAB], BF16, tag="slab")
-        h_slab = slabs.tile([P, SLAB], BF16, tag="slab")
-        for half in range(2):
-            load_half(first_slab, v0_rows[0, 0], half)
-            load_half(h_slab, pooled_sum, half)
-
-        h_codes = const.tile([P, SLAB_PASSES, P], U32, align_bytes=64)
-        h_scales = const.tile([P, SLAB_PASSES, P], U8, align_bytes=64)
-        for half in range(2):
-            nc.vector.tensor_scalar_mul(
-                out=h_slab[:, halves[half]], in0=h_slab[:, halves[half]], scalar1=per_count[:]
-            )
-            quantise_half(h_slab, half, h_codes, h_scales)
-
-        a0_grouped = const.tile([P, HIDDEN // K_PASS, P, 4], BF16, align_bytes=64)
-        for i in range(V0_SLABS):
-            slab = first_slab if i == 0 else slabs.tile([P, SLAB], BF16, tag="slab", name="slab")
-            sums = stats.tile([P, 2], F32)
-            for half in range(2):
-                if i > 0:
-                    load_half(slab, v0_rows[i // 2, i % 2], half)
-                sum_of_squares(slab[:, halves[half]], sums[:, half : half + 1])
-            row_scale = stats.tile([P, 1], F32)
-            nc.gpsimd.tensor_tensor(
-                out=row_scale[:], in0=sums[:, 0:1], in1=sums[:, 1:2], op=ALU.add
-            )
-            nc.gpsimd.tensor_tensor(
-                out=row_scale[:], in0=row_scale[:], in1=minus_half[:, 0:1], op=ALU.pow
-            )
-            nc.gpsimd.tensor_tensor(
-                out=row_scale[:], in0=row_scale[:], in1=gain0[:, i : i + 1], op=ALU.mult
-            )
-            w_codes = weights.tile([P, SLAB_PASSES, P], U32, align_bytes=64)
-            w_scales = weights.tile([P, SLAB_PASSES, P], U8, align_bytes=64)
-            for half in range(2):
-                nc.vector.tensor_scalar_mul(
-                    out=slab[:, halves[half]], in0=slab[:, halves[half]], scalar1=row_scale[:]
-                )
-                quantise_half(slab, half, w_codes, w_scales)
-            acc = psum_acc.tile([P, P], F32, tag="acc")
-            for n in range(SLAB_PASSES):
-                nc.tensor.matmul_mx(
-                    out=acc[:],
-                    lhsT=w_codes[:, n, :].bitcast(FP8X4),
-                    lhsT_scale=w_scales[:, n, :],
-                    rhs=h_codes[:, n, :].bitcast(FP8X4),
-                    rhs_scale=h_scales[:, n, :],
-                    start=(n == 0),
-                    stop=(n == SLAB_PASSES - 1),
-                )
+        def hidden_silu(s):
+            i = s - 1
             nc.scalar.activation(
                 out=a0_grouped[:, i // 4, :, i % 4],
-                in_=acc[:],
+                in_=product[s][:],
                 func=ACT.Silu,
                 bias=bias0[:, i : i + 1],
             )
 
-        a0_codes = const.tile([P, HIDDEN // K_PASS, P], U32, align_bytes=64)
-        a0_scales = const.tile([P, HIDDEN // K_PASS, P], U8, align_bytes=64)
-        nc.vector.quantize_mx(
-            out=a0_codes[:].rearrange("p n c -> p (n c)").bitcast(FP8X4),
-            scales=a0_scales[:].rearrange("p n c -> p (n c)"),
-            in_=a0_grouped[:].rearrange("p n c t -> p (n c t)"),
-        )
-
-        v1_rows = V1.rearrange("(i2 p e) k -> p i2 (e k)", p=P, e=2)
-        w1_slab = slabs.tile([P, SLAB], BF16, tag="slab")
-        w1_sums = stats.tile([P, V1_ROWS], F32)
-        for half in range(2):
-            nc.sync.dma_start(
-                out=w1_slab[:, halves[half]].rearrange("p (i2 w) -> p i2 w", i2=2),
-                in_=v1_rows[:, 2 * half : 2 * half + 2, :],
-            )
-        b1_all = const.tile([P, HIDDEN], BF16)
-        nc.sync.dma_start(out=b1_all[:], in_=b1.partition_broadcast(P))
-        for i in range(V1_ROWS):
-            sum_of_squares(w1_slab[:, i * HIDDEN : (i + 1) * HIDDEN], w1_sums[:, i : i + 1])
-        w1_scale = stats.tile([P, V1_ROWS], F32)
-        nc.gpsimd.tensor_tensor(out=w1_scale[:], in0=w1_sums[:], in1=minus_half[:], op=ALU.pow)
-        nc.gpsimd.tensor_tensor(out=w1_scale[:], in0=w1_scale[:], in1=gain1, op=ALU.mult)
-        w1_codes = const.tile([P, SLAB_PASSES, P], U32, align_bytes=64)
-        w1_scales = const.tile([P, SLAB_PASSES, P], U8, align_bytes=64)
-        for half in range(2):
-            for i in range(half * V1_ROWS // 2, (half + 1) * V1_ROWS // 2):
-                row = slice(i * HIDDEN, (i + 1) * HIDDEN)
-                nc.vector.tensor_scalar_mul(
-                    out=w1_slab[:, row], in0=w1_slab[:, row], scalar1=w1_scale[:, i : i + 1]
-                )
-            quantise_half(w1_slab, half, w1_codes, w1_scales)
-
-        passes = HIDDEN // K_PASS
-        for bank in range(2):
-            cols = slice(bank * 512, (bank + 1) * 512)
-            acc = psum_acc.tile([P, 512], F32, tag="acc")
-            for q in range(4):
-                i = 4 * bank + q
-                for n in range(passes):
-                    nc.tensor.matmul_mx(
-                        out=acc[:, q * P : (q + 1) * P],
-                        lhsT=a0_codes[:, n, :].bitcast(FP8X4),
-                        lhsT_scale=a0_scales[:, n, :],
-                        rhs=w1_codes[:, passes * i + n, :].bitcast(FP8X4),
-                        rhs_scale=w1_scales[:, passes * i + n, :],
-                        start=(n == 0),
-                        stop=(n == passes - 1),
-                    )
-            biased = final.tile([P, 512], F32)
+        def write_output(x):
+            cols = slice(x * BANK, (x + 1) * BANK)
+            biased = final.tile([P, BANK], F32, name="biased")
             nc.vector.tensor_tensor(
                 out=biased[:].rearrange("c (i2 p e) -> c i2 p e", i2=2, e=2),
-                in0=acc[:].rearrange("c (i2 e p) -> c i2 p e", i2=2, e=2),
+                in0=product[2 * V1_SLAB + x][:].rearrange("c (i2 e p) -> c i2 p e", i2=2, e=2),
                 in1=b1_all[:, cols].rearrange("c (i2 p e) -> c i2 p e", i2=2, e=2),
                 op=ALU.add,
             )
-            result = final.tile([P, 512], F32)
+            result = final.tile([P, BANK], F32, name="result")
             nc.scalar.activation(out=result[:], in_=biased[:], func=ACT.Silu)
             nc.sync.dma_start(out=out[:, cols], in_=result[:])
+
+        row_factors(1)
+        scale(0)
+        transposes(0)
+        for m in range(UNITS):
+            empty_banks(m)
+            if m + 1 < UNITS:
+                scale(m + 1)
+                transposes(m + 1)
+            if m % 2 == 0 and 1 <= m // 2 - 1 <= V0_SLABS:
+                hidden_silu(m // 2 - 1)
+            if m % 2 == 0 and m // 2 + LEAD < SLABS:
+                prepare(m // 2 + LEAD)
+            quantise(m)
+            multiply(m)
+        for x in range(2):
+            write_output(x)

@@ -50,7 +50,6 @@ def tile_hypernetfullyconnectedflexilayersizearch_pa_k_kernel(
         final = ctx.enter_context(tc.tile_pool(name="final", bufs=2))
         psum_t = ctx.enter_context(tc.psum_pool(name="psum_t", bufs=6))
         psum_acc = ctx.enter_context(tc.psum_pool(name="psum_acc", bufs=2))
-        ctx.enter_context(tc.manual_schedule())
         v0_rows = V0.rearrange("(i2 p e) (a w) -> i2 e p a w", p=P, e=2, a=4)
         dram_rows = {H_SLAB: pooled_sum.rearrange("c (a w) -> c a w", a=4)}
         for i in range(V0_SLABS):

@@ -50,6 +50,7 @@ def tile_hypernetfullyconnectedflexilayersizearch_pa_k_kernel(
         final = ctx.enter_context(tc.tile_pool(name="final", bufs=2))
         psum_t = ctx.enter_context(tc.psum_pool(name="psum_t", bufs=6))
         psum_acc = ctx.enter_context(tc.psum_pool(name="psum_acc", bufs=2))
+        ctx.enter_context(tc.manual_schedule())
         v0_rows = V0.rearrange("(i2 p e) (a w) -> i2 e p a w", p=P, e=2, a=4)
         dram_rows = {H_SLAB: pooled_sum.rearrange("c (a w) -> c a w", a=4)}
         for i in range(V0_SLABS):
@@ -75,6 +76,9 @@ def tile_hypernetfullyconnectedflexilayersizearch_pa_k_kernel(
                 in_=dram_rows[s][:, 2 * x : 2 * x + 2, :],
             )
 
+        new_slab(1)
+        fetch_half(1, 0)
+
         cnt = const.tile([P, 1], BF16)
         nc.sync.dma_start(out=cnt[:], in_=count)
         vec_rows = const.tile([P, P], F32)
@@ -85,11 +89,10 @@ def tile_hypernetfullyconnectedflexilayersizearch_pa_k_kernel(
                 in_=vec.rearrange("(r w) -> r w", r=4),
             )
 
-        new_slab(1)
         new_slab(H_SLAB)
-        for x in range(2):
-            fetch_half(1, x)
-            fetch_half(H_SLAB, x)
+        fetch_half(H_SLAB, 0)
+        fetch_half(1, 1)
+        fetch_half(H_SLAB, 1)
 
         ident = const.tile([P, P], F32)
         make_identity(nc, ident[:])
@@ -210,11 +213,13 @@ def tile_hypernetfullyconnectedflexilayersizearch_pa_k_kernel(
         def multiply(m):
             s, x = divmod(m, 2)
             if 1 <= s <= V0_SLABS:
-                if x == 0:
-                    product[s] = psum_acc.tile([P, P], F32, name="acc")
+                if x == 0 and (s - 1) % BANK_BLOCKS == 0:
+                    acc = psum_acc.tile([P, BANK_BLOCKS, P], F32, name="acc")
+                    for q in range(BANK_BLOCKS):
+                        product[s + q] = acc[:, q, :]
                 for n in range(HALF_PASSES * x, HALF_PASSES * (x + 1)):
                     nc.tensor.matmul_mx(
-                        out=product[s][:],
+                        out=product[s],
                         lhsT=codes[s][:, n, :].bitcast(FP8X4),
                         lhsT_scale=planes[s][:, n, :],
                         rhs=codes[H_SLAB][:, n, :].bitcast(FP8X4),
@@ -247,7 +252,7 @@ def tile_hypernetfullyconnectedflexilayersizearch_pa_k_kernel(
             i = s - 1
             nc.scalar.activation(
                 out=a0_grouped[:, i // 4, :, i % 4],
-                in_=product[s][:],
+                in_=product[s],
                 func=ACT.Silu,
                 bias=bias0[:, i : i + 1],
             )
@@ -273,8 +278,11 @@ def tile_hypernetfullyconnectedflexilayersizearch_pa_k_kernel(
             if m + 1 < UNITS:
                 scale(m + 1)
                 transposes(m + 1)
-            if m % 2 == 0 and 1 <= m // 2 - 1 <= V0_SLABS:
-                hidden_silu(m // 2 - 1)
+            if m == 2 * V0_SLABS:
+                for s in range(1, V0_SLABS):
+                    hidden_silu(s)
+            if m == 2 * V1_SLAB:
+                hidden_silu(V0_SLABS)
             if m % 2 == 0 and m // 2 + LEAD < SLABS:
                 prepare(m // 2 + LEAD)
             quantise(m)

@@ -18,20 +18,28 @@ K_PASS = 512
 BANK = 512
 
 SLAB = 8192
-HALF = SLAB // 2
+BANK_VALUES = 2 * BANK
+SLAB_BANKS = SLAB // BANK_VALUES
 SLAB_PASSES = SLAB // K_PASS
-HALF_PASSES = SLAB_PASSES // 2
-HALF_BANKS = HALF // 2 // BANK
+BANK_PASSES = SLAB_PASSES // SLAB_BANKS
 BANK_BLOCKS = BANK // P
 H_SLAB = 0
 V0_SLABS = HIDDEN // P
 V1_SLAB = V0_SLABS + 1
 SLABS = V1_SLAB + 1
-UNITS = 2 * SLABS
 V1_ROWS = SLAB // HIDDEN
 L1_PASSES = HIDDEN // K_PASS
 LEAD = 2
-SCALAR_UNITS = 3
+HALF_SLAB = ((0, 4), (4, 4))
+QUARTERS = ((0, 2), (2, 2), (4, 2), (6, 2))
+UNITS = (
+    [(H_SLAB, b, n) for b, n in QUARTERS]
+    + [(s, b, n) for s in range(1, V1_SLAB) for b, n in HALF_SLAB]
+    + [(V1_SLAB, 0, 4), (V1_SLAB, 4, 2), (V1_SLAB, 6, 2)]
+)
+V1_FIRST = UNITS.index((V1_SLAB, 0, 4))
+LAST = len(UNITS) - 1
+SCALAR_FROM = V1_FIRST - 2
 
 FLOPS = 2 * P * D_IN * HIDDEN + 2 * P * HIDDEN * HIDDEN
 
@@ -47,7 +55,7 @@ def tile_hypernetfullyconnectedflexilayersizearch_pa_k_kernel(
         stats = ctx.enter_context(tc.tile_pool(name="stats", bufs=4))
         regroup = ctx.enter_context(tc.tile_pool(name="regroup", bufs=3))
         weights = ctx.enter_context(tc.tile_pool(name="weights", bufs=2))
-        final = ctx.enter_context(tc.tile_pool(name="final", bufs=2))
+        final = ctx.enter_context(tc.tile_pool(name="final", bufs=3))
         psum_t = ctx.enter_context(tc.psum_pool(name="psum_t", bufs=6))
         psum_acc = ctx.enter_context(tc.psum_pool(name="psum_acc", bufs=2))
         ctx.enter_context(tc.manual_schedule())
@@ -68,19 +76,32 @@ def tile_hypernetfullyconnectedflexilayersizearch_pa_k_kernel(
         def new_slab(s):
             slab_tile[s] = slabs.tile([P, SLAB], BF16, name="slab")
 
-        def fetch_half(s, x):
-            nc.sync.dma_start(
-                out=slab_tile[s][:, x * HALF : (x + 1) * HALF].rearrange(
-                    "p (a w) -> p a w", a=2
-                ),
-                in_=dram_rows[s][:, 2 * x : 2 * x + 2, :],
-            )
+        def fetch(s, bank, n):
+            quarter, rest = divmod(bank, 2)
+            if n == 1:
+                src = dram_rows[s][:, quarter, rest * BANK_VALUES : (rest + 1) * BANK_VALUES]
+                dst = slab_tile[s][:, bank * BANK_VALUES : (bank + 1) * BANK_VALUES]
+            else:
+                src = dram_rows[s][:, quarter : quarter + n // 2, :]
+                dst = slab_tile[s][:, bank * BANK_VALUES : (bank + n) * BANK_VALUES].rearrange(
+                    "p (a w) -> p a w", a=n // 2
+                )
+            nc.sync.dma_start(out=dst, in_=src)
 
-        new_slab(1)
-        fetch_half(1, 0)
+        minus_half = const.tile([P, V1_ROWS], F32)
+        nc.vector.memset(minus_half[:], -0.5)
+        table_load = const.tile([P, 1], F32)
+        nc.scalar.activation(out=table_load[:], in_=minus_half[:, 0:1], func=ACT.Silu)
+
+        for s in (1, H_SLAB, 2):
+            new_slab(s)
+        fetch(1, 0, 1)
 
         cnt = const.tile([P, 1], BF16)
         nc.sync.dma_start(out=cnt[:], in_=count)
+        fetch(1, 1, 1)
+        fetch(H_SLAB, 0, 2)
+        fetch(1, 2, 2)
         vec_rows = const.tile([P, P], F32)
         nc.vector.memset(vec_rows[:], 0.0)
         for n, vec in enumerate((g0, b0, g1)):
@@ -89,20 +110,19 @@ def tile_hypernetfullyconnectedflexilayersizearch_pa_k_kernel(
                 in_=vec.rearrange("(r w) -> r w", r=4),
             )
 
-        new_slab(H_SLAB)
-        fetch_half(H_SLAB, 0)
-        fetch_half(1, 1)
-        fetch_half(H_SLAB, 1)
+        fetch(H_SLAB, 2, 2)
+        fetch(1, 4, 2)
+        fetch(H_SLAB, 4, 2)
+        fetch(1, 6, 2)
+        fetch(2, 0, 2)
+        fetch(H_SLAB, 6, 2)
+        fetch(2, 2, 2)
+        fetch(2, 4, 4)
 
         ident = const.tile([P, P], F32)
         make_identity(nc, ident[:])
-        minus_half = const.tile([P, V1_ROWS], F32)
-        nc.vector.memset(minus_half[:], -0.5)
 
-        vec_t = psum_t.tile([P, P], F32, tag="xt")
-        nc.tensor.transpose(vec_t[:], vec_rows[:], ident[:])
         vecs = const.tile([P, 3 * V0_SLABS], F32)
-        nc.vector.tensor_copy(out=vecs[:], in_=vec_t[:, 0:12].bitcast(BF16))
         bias0 = vecs[:, V0_SLABS : 2 * V0_SLABS]
         gain = {V1_SLAB: vecs[:, 2 * V0_SLABS : 3 * V0_SLABS]}
         for i in range(V0_SLABS):
@@ -114,50 +134,69 @@ def tile_hypernetfullyconnectedflexilayersizearch_pa_k_kernel(
         nc.vector.reciprocal(out=per_count[:], in_=per_count[:])
         factor[H_SLAB] = per_count[:]
 
-        def row_factors(s):
-            rows = gain[s].shape[1]
-            piece = min(SLAB // rows, HALF)
-            sums = stats.tile([P, SLAB // piece], F32, name="sums%d" % rows)
-            factor[s] = stats.tile([P, rows], F32, name="factor%d" % rows)[:]
-            for x in range(2):
-                for n in range(x * HALF // piece, (x + 1) * HALF // piece):
-                    squares = scratch.tile([P, HALF], BF16, name="squares")
-                    nc.scalar.activation(
-                        out=squares[:, 0:piece],
-                        in_=slab_tile[s][:, n * piece : (n + 1) * piece],
-                        func=ACT.Square,
-                        accum_out=sums[:, n : n + 1],
-                    )
-                if rows == 1 and x == 0:
-                    continue
-                if rows == 1:
-                    mine = factor[s]
+        def square(s, bank, n, total):
+            squares = scratch.tile([P, SLAB // 2], BF16, name="squares")
+            nc.scalar.activation(
+                out=squares[:, 0 : n * BANK_VALUES],
+                in_=slab_tile[s][:, bank * BANK_VALUES : (bank + n) * BANK_VALUES],
+                func=ACT.Square,
+                accum_out=total,
+            )
+
+        def gain_over_length(result, lengths, gains):
+            width = result.shape[1]
+            nc.gpsimd.tensor_tensor(
+                out=result, in0=lengths, in1=minus_half[:, 0:width], op=ALU.pow
+            )
+            nc.gpsimd.tensor_tensor(out=result, in0=result, in1=gains, op=ALU.mult)
+
+        def v0_factors(s, pieces):
+            sums = stats.tile([P, SLAB_BANKS], F32, name="sums")
+            factor[s] = stats.tile([P, 1], F32, name="factor")[:]
+            bank = 0
+            for i, n in enumerate(pieces):
+                square(s, bank, n, sums[:, i : i + 1])
+                bank += n
+                if i > 0:
                     nc.gpsimd.tensor_tensor(
-                        out=mine, in0=sums[:, 0:1], in1=sums[:, 1:2], op=ALU.add
+                        out=factor[s],
+                        in0=sums[:, 0:1] if i == 1 else factor[s],
+                        in1=sums[:, i : i + 1],
+                        op=ALU.add,
                     )
-                    lengths, gains = mine, gain[s]
-                else:
-                    cols = slice(x * rows // 2, (x + 1) * rows // 2)
-                    mine, lengths, gains = factor[s][:, cols], sums[:, cols], gain[s][:, cols]
-                width = mine.shape[1]
-                nc.gpsimd.tensor_tensor(
-                    out=mine, in0=lengths, in1=minus_half[:, 0:width], op=ALU.pow
-                )
-                nc.gpsimd.tensor_tensor(out=mine, in0=mine, in1=gains, op=ALU.mult)
+            gain_over_length(factor[s], factor[s], gain[s])
+
+        v1_sums = const.tile([P, V1_ROWS], F32)
+        factor[V1_SLAB] = const.tile([P, V1_ROWS], F32, name="v1_factor")[:]
+
+        def v1_factors(first, n):
+            for bank in range(first, first + n):
+                square(V1_SLAB, bank, 1, v1_sums[:, bank : bank + 1])
+            cols = slice(first, first + n)
+            gain_over_length(factor[V1_SLAB][:, cols], v1_sums[:, cols], gain[V1_SLAB][:, cols])
+
+        def fetch_slab(s):
+            new_slab(s)
+            for bank in range(0, SLAB_BANKS, 4):
+                fetch(s, bank, 4)
 
         def prepare(s):
-            new_slab(s)
-            for x in range(2):
-                fetch_half(s, x)
+            if s == 2:
+                v0_factors(s, (2, 2, 4))
+                return
+            fetch_slab(s)
             if s == V1_SLAB:
                 nc.sync.dma_start(out=b1_all[:], in_=b1.partition_broadcast(P))
-            row_factors(s)
+                v1_factors(0, 4)
+                v1_factors(4, 4)
+            else:
+                v0_factors(s, (4, 4))
 
         def scale(m):
-            s, x = divmod(m, 2)
+            s, b, n = UNITS[m]
             span = SLAB // factor[s].shape[1]
-            piece = min(span, HALF)
-            for start in range(x * HALF, (x + 1) * HALF, piece):
+            piece = min(span, n * BANK_VALUES)
+            for start in range(b * BANK_VALUES, (b + n) * BANK_VALUES, piece):
                 values = slab_tile[s][:, start : start + piece]
                 nc.vector.tensor_scalar_mul(
                     out=values,
@@ -166,31 +205,35 @@ def tile_hypernetfullyconnectedflexilayersizearch_pa_k_kernel(
                 )
 
         def transposes(m):
-            s, x = divmod(m, 2)
+            s, first, n = UNITS[m]
             words = slab_tile[s][:].bitcast(F32)
             banks[m] = []
-            for b in range(HALF_BANKS):
+            for b in range(first, first + n):
                 xt = psum_t.tile([P, BANK_BLOCKS, P], F32, name="xt")
                 for i in range(BANK_BLOCKS):
-                    block = BANK_BLOCKS * (HALF_BANKS * x + b) + i
+                    block = BANK_BLOCKS * b + i
                     nc.tensor.transpose(
                         xt[:, i, :], words[:, block * P : (block + 1) * P], ident[:]
                     )
                 banks[m].append(xt)
 
         def empty_banks(m):
-            grouped[m] = regroup.tile([P, HALF_PASSES, P, 2], F32, name="grouped", align_bytes=64)
+            n = UNITS[m][2]
+            grouped[m] = regroup.tile(
+                [P, n * BANK_PASSES, P, 2], F32, tag="grouped", name="grouped", align_bytes=64
+            )
+            by_scalar = 0 if m < SCALAR_FROM else n if m < V1_FIRST else n // 2
             for b, xt in enumerate(banks[m]):
-                target = grouped[m][:, 2 * b : 2 * b + 2, :, :]
+                target = grouped[m][:, BANK_PASSES * b : BANK_PASSES * (b + 1), :, :]
                 planes_uv = xt[:].rearrange("p (n u) r -> p n r u", u=2)
-                if m >= UNITS - SCALAR_UNITS:
+                if b >= n - by_scalar:
                     nc.scalar.copy(out=target, in_=planes_uv)
                 else:
                     nc.vector.tensor_copy(out=target, in_=planes_uv)
 
         def quantise(m):
-            s, x = divmod(m, 2)
-            if x == 0:
+            s, first, n = UNITS[m]
+            if first == 0:
                 pool = weights if 1 <= s <= V0_SLABS else const
                 label = "w0" if 1 <= s <= V0_SLABS else "slab%d" % s
                 codes[s] = pool.tile(
@@ -199,7 +242,7 @@ def tile_hypernetfullyconnectedflexilayersizearch_pa_k_kernel(
                 planes[s] = pool.tile(
                     [P, SLAB_PASSES, P], U8, name=label + "_planes", align_bytes=64
                 )
-            passes = slice(HALF_PASSES * x, HALF_PASSES * (x + 1))
+            passes = slice(BANK_PASSES * first, BANK_PASSES * (first + n))
             nc.vector.quantize_mx(
                 out=codes[s][:, passes, :].rearrange("p n r -> p (n r)").bitcast(FP8X4),
                 scales=planes[s][:, passes, :].rearrange("p n r -> p (n r)"),
@@ -211,13 +254,13 @@ def tile_hypernetfullyconnectedflexilayersizearch_pa_k_kernel(
         a0_planes = const.tile([P, L1_PASSES, P], U8, align_bytes=64)
 
         def multiply(m):
-            s, x = divmod(m, 2)
+            s, first, banks_here = UNITS[m]
             if 1 <= s <= V0_SLABS:
-                if x == 0 and (s - 1) % BANK_BLOCKS == 0:
+                if first == 0 and (s - 1) % BANK_BLOCKS == 0:
                     acc = psum_acc.tile([P, BANK_BLOCKS, P], F32, name="acc")
                     for q in range(BANK_BLOCKS):
                         product[s + q] = acc[:, q, :]
-                for n in range(HALF_PASSES * x, HALF_PASSES * (x + 1)):
+                for n in range(BANK_PASSES * first, BANK_PASSES * (first + banks_here)):
                     nc.tensor.matmul_mx(
                         out=product[s],
                         lhsT=codes[s][:, n, :].bitcast(FP8X4),
@@ -228,18 +271,12 @@ def tile_hypernetfullyconnectedflexilayersizearch_pa_k_kernel(
                         stop=(n == SLAB_PASSES - 1),
                     )
             if s == V1_SLAB:
-                if x == 0:
-                    nc.vector.quantize_mx(
-                        out=a0_codes[:].rearrange("p n c -> p (n c)").bitcast(FP8X4),
-                        scales=a0_planes[:].rearrange("p n c -> p (n c)"),
-                        in_=a0_grouped[:].rearrange("p n c t -> p (n c t)"),
-                    )
                 product[m] = psum_t.tile([P, BANK], F32, tag="xt", name="out_bank")
-                for q in range(V1_ROWS // 2):
-                    i = x * V1_ROWS // 2 + q
+                for i in range(first, first + banks_here):
+                    cols = slice((i - first) * P, (i - first + 1) * P)
                     for n in range(L1_PASSES):
                         nc.tensor.matmul_mx(
-                            out=product[m][:, q * P : (q + 1) * P],
+                            out=product[m][:, cols],
                             lhsT=a0_codes[:, n, :].bitcast(FP8X4),
                             lhsT_scale=a0_planes[:, n, :],
                             rhs=codes[s][:, L1_PASSES * i + n, :].bitcast(FP8X4),
@@ -247,6 +284,13 @@ def tile_hypernetfullyconnectedflexilayersizearch_pa_k_kernel(
                             start=(n == 0),
                             stop=(n == L1_PASSES - 1),
                         )
+
+        def quantise_hidden():
+            nc.vector.quantize_mx(
+                out=a0_codes[:].rearrange("p n c -> p (n c)").bitcast(FP8X4),
+                scales=a0_planes[:].rearrange("p n c -> p (n c)"),
+                in_=a0_grouped[:].rearrange("p n c t -> p (n c t)"),
+            )
 
         def hidden_silu(s):
             i = s - 1
@@ -257,35 +301,46 @@ def tile_hypernetfullyconnectedflexilayersizearch_pa_k_kernel(
                 bias=bias0[:, i : i + 1],
             )
 
-        def write_output(x):
-            cols = slice(x * BANK, (x + 1) * BANK)
+        def write_output(m):
+            s, first, n = UNITS[m]
+            width = n * P
+            cols = slice(first * P, first * P + width)
             biased = final.tile([P, BANK], F32, name="biased")
             nc.vector.tensor_tensor(
-                out=biased[:].rearrange("c (i2 p e) -> c i2 p e", i2=2, e=2),
-                in0=product[2 * V1_SLAB + x][:].rearrange("c (i2 e p) -> c i2 p e", i2=2, e=2),
-                in1=b1_all[:, cols].rearrange("c (i2 p e) -> c i2 p e", i2=2, e=2),
+                out=biased[:, 0:width].rearrange("c (i2 p e) -> c i2 p e", p=P, e=2),
+                in0=product[m][:, 0:width].rearrange("c (i2 e p) -> c i2 p e", p=P, e=2),
+                in1=b1_all[:, cols].rearrange("c (i2 p e) -> c i2 p e", p=P, e=2),
                 op=ALU.add,
             )
             result = final.tile([P, BANK], F32, name="result")
-            nc.scalar.activation(out=result[:], in_=biased[:], func=ACT.Silu)
-            nc.sync.dma_start(out=out[:, cols], in_=result[:])
+            nc.scalar.activation(out=result[:, 0:width], in_=biased[:, 0:width], func=ACT.Silu)
+            nc.sync.dma_start(out=out[:, cols], in_=result[:, 0:width])
 
-        row_factors(1)
         scale(0)
         transposes(0)
-        for m in range(UNITS):
+        scaled = 0
+        vec_t = psum_t.tile([P, P], F32, tag="xt")
+        nc.tensor.transpose(vec_t[:], vec_rows[:], ident[:])
+        for m, (s, first, n) in enumerate(UNITS):
             empty_banks(m)
-            if m + 1 < UNITS:
-                scale(m + 1)
-                transposes(m + 1)
-            if m == 2 * V0_SLABS:
-                for s in range(1, V0_SLABS):
-                    hidden_silu(s)
-            if m == 2 * V1_SLAB:
-                hidden_silu(V0_SLABS)
-            if m % 2 == 0 and m // 2 + LEAD < SLABS:
-                prepare(m // 2 + LEAD)
+            ahead = 2 if m + 1 >= SCALAR_FROM else 1
+            while scaled < min(m + ahead, LAST):
+                scaled += 1
+                scale(scaled)
+                transposes(scaled)
+            if m == V1_FIRST:
+                for done in range(1, V0_SLABS + 1):
+                    hidden_silu(done)
+            if m == 0:
+                nc.vector.tensor_copy(out=vecs[:], in_=vec_t[:, 0:12].bitcast(BF16))
+                v0_factors(1, (1, 1, 2, 2, 2))
+            if first == 0 and s + LEAD <= V1_SLAB:
+                prepare(s + LEAD)
+            if m == V1_FIRST + 1:
+                quantise_hidden()
+                multiply(V1_FIRST)
             quantise(m)
-            multiply(m)
-        for x in range(2):
-            write_output(x)
+            if m != V1_FIRST:
+                multiply(m)
+        for m in range(V1_FIRST, LAST + 1):
+            write_output(m)

@@ -100,8 +100,9 @@ def tile_hypernetfullyconnectedflexilayersizearch_pa_k_kernel(
         cnt = const.tile([P, 1], BF16)
         nc.sync.dma_start(out=cnt[:], in_=count)
         fetch(1, 1, 1)
+        fetch(1, 2, 1)
         fetch(H_SLAB, 0, 2)
-        fetch(1, 2, 2)
+        fetch(1, 3, 1)
         vec_rows = const.tile([P, P], F32)
         nc.vector.memset(vec_rows[:], 0.0)
         for n, vec in enumerate((g0, b0, g1)):
@@ -110,10 +111,10 @@ def tile_hypernetfullyconnectedflexilayersizearch_pa_k_kernel(
                 in_=vec.rearrange("(r w) -> r w", r=4),
             )
 
-        fetch(H_SLAB, 2, 2)
         fetch(1, 4, 2)
-        fetch(H_SLAB, 4, 2)
+        fetch(H_SLAB, 2, 2)
         fetch(1, 6, 2)
+        fetch(H_SLAB, 4, 2)
         fetch(2, 0, 2)
         fetch(H_SLAB, 6, 2)
         fetch(2, 2, 2)
@@ -143,6 +144,19 @@ def tile_hypernetfullyconnectedflexilayersizearch_pa_k_kernel(
                 accum_out=total,
             )
 
+        def square_on_vector(s, bank, total):
+            squares = scratch.tile([P, BANK_VALUES], BF16, name="vector_squares")
+            values = slab_tile[s][:, bank * BANK_VALUES : (bank + 1) * BANK_VALUES]
+            nc.vector.scalar_tensor_tensor(
+                out=squares[:],
+                in0=values,
+                scalar=1.0,
+                in1=values,
+                op0=ALU.mult,
+                op1=ALU.mult,
+                accum_out=total,
+            )
+
         def gain_over_length(result, lengths, gains):
             width = result.shape[1]
             nc.gpsimd.tensor_tensor(
@@ -151,11 +165,12 @@ def tile_hypernetfullyconnectedflexilayersizearch_pa_k_kernel(
             nc.gpsimd.tensor_tensor(out=result, in0=result, in1=gains, op=ALU.mult)
 
         def v0_factors(s, pieces):
-            sums = stats.tile([P, SLAB_BANKS], F32, name="sums")
+            sums = slab1_sums if s == 1 else stats.tile([P, SLAB_BANKS], F32, name="sums")
             factor[s] = stats.tile([P, 1], F32, name="factor")[:]
             bank = 0
             for i, n in enumerate(pieces):
-                square(s, bank, n, sums[:, i : i + 1])
+                if (s, bank) != (1, 1):
+                    square(s, bank, n, sums[:, i : i + 1])
                 bank += n
                 if i > 0:
                     nc.gpsimd.tensor_tensor(
@@ -166,6 +181,7 @@ def tile_hypernetfullyconnectedflexilayersizearch_pa_k_kernel(
                     )
             gain_over_length(factor[s], factor[s], gain[s])
 
+        slab1_sums = const.tile([P, SLAB_BANKS], F32)
         v1_sums = const.tile([P, V1_ROWS], F32)
         factor[V1_SLAB] = const.tile([P, V1_ROWS], F32, name="v1_factor")[:]
 
@@ -222,11 +238,10 @@ def tile_hypernetfullyconnectedflexilayersizearch_pa_k_kernel(
             grouped[m] = regroup.tile(
                 [P, n * BANK_PASSES, P, 2], F32, tag="grouped", name="grouped", align_bytes=64
             )
-            by_scalar = 0 if m < SCALAR_FROM else n if m < V1_FIRST else n // 2
             for b, xt in enumerate(banks[m]):
                 target = grouped[m][:, BANK_PASSES * b : BANK_PASSES * (b + 1), :, :]
                 planes_uv = xt[:].rearrange("p (n u) r -> p n r u", u=2)
-                if b >= n - by_scalar:
+                if m >= SCALAR_FROM:
                     nc.scalar.copy(out=target, in_=planes_uv)
                 else:
                     nc.vector.tensor_copy(out=target, in_=planes_uv)
@@ -249,6 +264,7 @@ def tile_hypernetfullyconnectedflexilayersizearch_pa_k_kernel(
                 in_=grouped[m][:].rearrange("p n r u -> p (n r u)").bitcast(BF16),
             )
 
+        a0_rows = const.tile([P, V0_SLABS, P], BF16)
         a0_grouped = const.tile([P, L1_PASSES, P, 4], BF16, align_bytes=64)
         a0_codes = const.tile([P, L1_PASSES, P], U32, align_bytes=64)
         a0_planes = const.tile([P, L1_PASSES, P], U8, align_bytes=64)
@@ -285,6 +301,12 @@ def tile_hypernetfullyconnectedflexilayersizearch_pa_k_kernel(
                             stop=(n == L1_PASSES - 1),
                         )
 
+        def group_hidden(n):
+            nc.vector.tensor_copy(
+                out=a0_grouped[:, n, :, :],
+                in_=a0_rows[:, 4 * n : 4 * n + 4, :].rearrange("p t c -> p c t"),
+            )
+
         def quantise_hidden():
             nc.vector.quantize_mx(
                 out=a0_codes[:].rearrange("p n c -> p (n c)").bitcast(FP8X4),
@@ -295,7 +317,7 @@ def tile_hypernetfullyconnectedflexilayersizearch_pa_k_kernel(
         def hidden_silu(s):
             i = s - 1
             nc.scalar.activation(
-                out=a0_grouped[:, i // 4, :, i % 4],
+                out=a0_rows[:, i, :],
                 in_=product[s],
                 func=ACT.Silu,
                 bias=bias0[:, i : i + 1],
@@ -316,6 +338,7 @@ def tile_hypernetfullyconnectedflexilayersizearch_pa_k_kernel(
             nc.scalar.activation(out=result[:, 0:width], in_=biased[:, 0:width], func=ACT.Silu)
             nc.sync.dma_start(out=out[:, cols], in_=result[:, 0:width])
 
+        square_on_vector(1, 1, slab1_sums[:, 1:2])
         scale(0)
         transposes(0)
         scaled = 0
@@ -323,7 +346,7 @@ def tile_hypernetfullyconnectedflexilayersizearch_pa_k_kernel(
         nc.tensor.transpose(vec_t[:], vec_rows[:], ident[:])
         for m, (s, first, n) in enumerate(UNITS):
             empty_banks(m)
-            ahead = 2 if m + 1 >= SCALAR_FROM else 1
+            ahead = 2 if m + 2 >= SCALAR_FROM else 1
             while scaled < min(m + ahead, LAST):
                 scaled += 1
                 scale(scaled)
@@ -333,13 +356,15 @@ def tile_hypernetfullyconnectedflexilayersizearch_pa_k_kernel(
                     hidden_silu(done)
             if m == 0:
                 nc.vector.tensor_copy(out=vecs[:], in_=vec_t[:, 0:12].bitcast(BF16))
-                v0_factors(1, (1, 1, 2, 2, 2))
+                v0_factors(1, (1, 1, 1, 1, 2, 2))
             if first == 0 and s + LEAD <= V1_SLAB:
                 prepare(s + LEAD)
+            if m in (V1_FIRST, V1_FIRST + 1):
+                group_hidden(m - V1_FIRST)
+            quantise(m)
             if m == V1_FIRST + 1:
                 quantise_hidden()
                 multiply(V1_FIRST)
-            quantise(m)
             if m != V1_FIRST:
                 multiply(m)
         for m in range(V1_FIRST, LAST + 1):

@@ -136,7 +136,7 @@ def tile_hypernetfullyconnectedflexilayersizearch_pa_k_kernel(
         factor[H_SLAB] = per_count[:]
 
         def square(s, bank, n, total):
-            squares = scratch.tile([P, SLAB // 2], BF16, name="squares")
+            squares = scratch.tile([P, SLAB], BF16, name="squares")
             nc.scalar.activation(
                 out=squares[:, 0 : n * BANK_VALUES],
                 in_=slab_tile[s][:, bank * BANK_VALUES : (bank + n) * BANK_VALUES],
@@ -157,12 +157,11 @@ def tile_hypernetfullyconnectedflexilayersizearch_pa_k_kernel(
                 accum_out=total,
             )
 
-        def gain_over_length(result, lengths, gains):
+        def one_over_length(result, lengths):
             width = result.shape[1]
             nc.gpsimd.tensor_tensor(
                 out=result, in0=lengths, in1=minus_half[:, 0:width], op=ALU.pow
             )
-            nc.gpsimd.tensor_tensor(out=result, in0=result, in1=gains, op=ALU.mult)
 
         def v0_factors(s, pieces):
             sums = slab1_sums if s == 1 else stats.tile([P, SLAB_BANKS], F32, name="sums")
@@ -179,7 +178,7 @@ def tile_hypernetfullyconnectedflexilayersizearch_pa_k_kernel(
                         in1=sums[:, i : i + 1],
                         op=ALU.add,
                     )
-            gain_over_length(factor[s], factor[s], gain[s])
+            one_over_length(factor[s], factor[s] if len(pieces) > 1 else sums[:, 0:1])
 
         slab1_sums = const.tile([P, SLAB_BANKS], F32)
         v1_sums = const.tile([P, V1_ROWS], F32)
@@ -189,7 +188,7 @@ def tile_hypernetfullyconnectedflexilayersizearch_pa_k_kernel(
             for bank in range(first, first + n):
                 square(V1_SLAB, bank, 1, v1_sums[:, bank : bank + 1])
             cols = slice(first, first + n)
-            gain_over_length(factor[V1_SLAB][:, cols], v1_sums[:, cols], gain[V1_SLAB][:, cols])
+            one_over_length(factor[V1_SLAB][:, cols], v1_sums[:, cols])
 
         def fetch_slab(s):
             new_slab(s)
@@ -206,7 +205,7 @@ def tile_hypernetfullyconnectedflexilayersizearch_pa_k_kernel(
                 v1_factors(0, 4)
                 v1_factors(4, 4)
             else:
-                v0_factors(s, (4, 4))
+                v0_factors(s, (8,))
 
         def scale(m):
             s, b, n = UNITS[m]
@@ -214,11 +213,20 @@ def tile_hypernetfullyconnectedflexilayersizearch_pa_k_kernel(
             piece = min(span, n * BANK_VALUES)
             for start in range(b * BANK_VALUES, (b + n) * BANK_VALUES, piece):
                 values = slab_tile[s][:, start : start + piece]
-                nc.vector.tensor_scalar_mul(
-                    out=values,
-                    in0=values,
-                    scalar1=factor[s][:, start // span : start // span + 1],
-                )
+                row = slice(start // span, start // span + 1)
+                if s == H_SLAB:
+                    nc.vector.tensor_scalar_mul(
+                        out=values, in0=values, scalar1=factor[s][:, row]
+                    )
+                else:
+                    nc.vector.tensor_scalar(
+                        out=values,
+                        in0=values,
+                        scalar1=factor[s][:, row],
+                        scalar2=gain[s][:, row],
+                        op0=ALU.mult,
+                        op1=ALU.mult,
+                    )
 
         def transposes(m):
             s, first, n = UNITS[m]

@@ -95,13 +95,15 @@ def tile_hypernetfullyconnectedflexilayersizearch_pa_k_kernel(
 
         for s in (1, H_SLAB, 2):
             new_slab(s)
-        fetch(1, 0, 1)
 
         cnt = const.tile([P, 1], BF16)
         nc.sync.dma_start(out=cnt[:], in_=count)
+        fetch(H_SLAB, 0, 1)
+        fetch(1, 0, 1)
+        fetch(H_SLAB, 1, 1)
         fetch(1, 1, 1)
         fetch(1, 2, 1)
-        fetch(H_SLAB, 0, 2)
+        fetch(H_SLAB, 2, 2)
         fetch(1, 3, 1)
         vec_rows = const.tile([P, P], F32)
         nc.vector.memset(vec_rows[:], 0.0)
@@ -111,12 +113,13 @@ def tile_hypernetfullyconnectedflexilayersizearch_pa_k_kernel(
                 in_=vec.rearrange("(r w) -> r w", r=4),
             )
 
-        fetch(1, 4, 2)
-        fetch(H_SLAB, 2, 2)
-        fetch(1, 6, 2)
+        fetch(1, 4, 1)
         fetch(H_SLAB, 4, 2)
-        fetch(2, 0, 2)
+        fetch(1, 5, 1)
+        fetch(1, 6, 1)
         fetch(H_SLAB, 6, 2)
+        fetch(1, 7, 1)
+        fetch(2, 0, 2)
         fetch(2, 2, 2)
         fetch(2, 4, 4)
 
@@ -144,19 +147,6 @@ def tile_hypernetfullyconnectedflexilayersizearch_pa_k_kernel(
                 accum_out=total,
             )
 
-        def square_on_vector(s, bank, total):
-            squares = scratch.tile([P, BANK_VALUES], BF16, name="vector_squares")
-            values = slab_tile[s][:, bank * BANK_VALUES : (bank + 1) * BANK_VALUES]
-            nc.vector.scalar_tensor_tensor(
-                out=squares[:],
-                in0=values,
-                scalar=1.0,
-                in1=values,
-                op0=ALU.mult,
-                op1=ALU.mult,
-                accum_out=total,
-            )
-
         def one_over_length(result, lengths):
             width = result.shape[1]
             nc.gpsimd.tensor_tensor(
@@ -164,12 +154,11 @@ def tile_hypernetfullyconnectedflexilayersizearch_pa_k_kernel(
             )
 
         def v0_factors(s, pieces):
-            sums = slab1_sums if s == 1 else stats.tile([P, SLAB_BANKS], F32, name="sums")
+            sums = stats.tile([P, SLAB_BANKS], F32, name="sums")
             factor[s] = stats.tile([P, 1], F32, name="factor")[:]
             bank = 0
             for i, n in enumerate(pieces):
-                if (s, bank) != (1, 1):
-                    square(s, bank, n, sums[:, i : i + 1])
+                square(s, bank, n, sums[:, i : i + 1])
                 bank += n
                 if i > 0:
                     nc.gpsimd.tensor_tensor(
@@ -180,7 +169,6 @@ def tile_hypernetfullyconnectedflexilayersizearch_pa_k_kernel(
                     )
             one_over_length(factor[s], factor[s] if len(pieces) > 1 else sums[:, 0:1])
 
-        slab1_sums = const.tile([P, SLAB_BANKS], F32)
         v1_sums = const.tile([P, V1_ROWS], F32)
         factor[V1_SLAB] = const.tile([P, V1_ROWS], F32, name="v1_factor")[:]
 
@@ -210,7 +198,7 @@ def tile_hypernetfullyconnectedflexilayersizearch_pa_k_kernel(
         def scale(m):
             s, b, n = UNITS[m]
             span = SLAB // factor[s].shape[1]
-            piece = min(span, n * BANK_VALUES)
+            piece = min(span, BANK_VALUES if m == 0 else n * BANK_VALUES)
             for start in range(b * BANK_VALUES, (b + n) * BANK_VALUES, piece):
                 values = slab_tile[s][:, start : start + piece]
                 row = slice(start // span, start // span + 1)
@@ -346,12 +334,9 @@ def tile_hypernetfullyconnectedflexilayersizearch_pa_k_kernel(
             nc.scalar.activation(out=result[:, 0:width], in_=biased[:, 0:width], func=ACT.Silu)
             nc.sync.dma_start(out=out[:, cols], in_=result[:, 0:width])
 
-        square_on_vector(1, 1, slab1_sums[:, 1:2])
         scale(0)
         transposes(0)
         scaled = 0
-        vec_t = psum_t.tile([P, P], F32, tag="xt")
-        nc.tensor.transpose(vec_t[:], vec_rows[:], ident[:])
         for m, (s, first, n) in enumerate(UNITS):
             empty_banks(m)
             ahead = 2 if m + 2 >= SCALAR_FROM else 1
@@ -363,8 +348,12 @@ def tile_hypernetfullyconnectedflexilayersizearch_pa_k_kernel(
                 for done in range(1, V0_SLABS + 1):
                     hidden_silu(done)
             if m == 0:
+                v0_factors(1, (1,) * SLAB_BANKS)
+            if m == 1:
+                vec_t = psum_t.tile([P, P], F32, tag="xt")
+                nc.tensor.transpose(vec_t[:], vec_rows[:], ident[:])
+            if m == 2:
                 nc.vector.tensor_copy(out=vecs[:], in_=vec_t[:, 0:12].bitcast(BF16))
-                v0_factors(1, (1, 1, 1, 1, 2, 2))
             if first == 0 and s + LEAD <= V1_SLAB:
                 prepare(s + LEAD)
             if m in (V1_FIRST, V1_FIRST + 1):

@@ -237,7 +237,7 @@ def tile_hypernetfullyconnectedflexilayersizearch_pa_k_kernel(
             for b, xt in enumerate(banks[m]):
                 target = grouped[m][:, BANK_PASSES * b : BANK_PASSES * (b + 1), :, :]
                 planes_uv = xt[:].rearrange("p (n u) r -> p n r u", u=2)
-                if m >= SCALAR_FROM:
+                if m > SCALAR_FROM or (m == SCALAR_FROM and b >= n // 2):
                     nc.scalar.copy(out=target, in_=planes_uv)
                 else:
                     nc.vector.tensor_copy(out=target, in_=planes_uv)
@@ -356,13 +356,12 @@ def tile_hypernetfullyconnectedflexilayersizearch_pa_k_kernel(
                 nc.vector.tensor_copy(out=vecs[:], in_=vec_t[:, 0:12].bitcast(BF16))
             if first == 0 and s + LEAD <= V1_SLAB:
                 prepare(s + LEAD)
-            if m in (V1_FIRST, V1_FIRST + 1):
-                group_hidden(m - V1_FIRST)
+            if m == V1_FIRST:
+                group_hidden(0)
             quantise(m)
-            if m == V1_FIRST + 1:
+            if m == V1_FIRST:
+                group_hidden(1)
                 quantise_hidden()
-                multiply(V1_FIRST)
-            if m != V1_FIRST:
-                multiply(m)
+            multiply(m)
         for m in range(V1_FIRST, LAST + 1):
             write_output(m)

@@ -39,7 +39,10 @@ UNITS = (
 )
 V1_FIRST = UNITS.index((V1_SLAB, 0, 4))
 LAST = len(UNITS) - 1
-SCALAR_FROM = V1_FIRST - 2
+GRAM_SLAB = 6
+GRAM_BANKS = SLAB_BANKS - 1
+GRAM_FROM = UNITS.index((1, 0, 4))
+SCALAR_FROM = V1_FIRST - 4
 
 FLOPS = 2 * P * D_IN * HIDDEN + 2 * P * HIDDEN * HIDDEN
 
@@ -50,14 +53,15 @@ def tile_hypernetfullyconnectedflexilayersizearch_pa_k_kernel(
     nc = tc.nc
     with ExitStack() as ctx:
         const = ctx.enter_context(tc.tile_pool(name="const", bufs=1))
-        slabs = ctx.enter_context(tc.tile_pool(name="slabs", bufs=5))
+        slabs = ctx.enter_context(tc.tile_pool(name="slabs", bufs=6))
         scratch = ctx.enter_context(tc.tile_pool(name="scratch", bufs=2))
+        unread = ctx.enter_context(tc.tile_pool(name="unread", bufs=2))
         stats = ctx.enter_context(tc.tile_pool(name="stats", bufs=4))
         regroup = ctx.enter_context(tc.tile_pool(name="regroup", bufs=3))
         weights = ctx.enter_context(tc.tile_pool(name="weights", bufs=2))
         final = ctx.enter_context(tc.tile_pool(name="final", bufs=3))
         psum_t = ctx.enter_context(tc.psum_pool(name="psum_t", bufs=6))
-        psum_acc = ctx.enter_context(tc.psum_pool(name="psum_acc", bufs=2))
+        psum_acc = ctx.enter_context(tc.psum_pool(name="psum_acc", bufs=1))
         ctx.enter_context(tc.manual_schedule())
         v0_rows = V0.rearrange("(i2 p e) (a w) -> i2 e p a w", p=P, e=2, a=4)
         dram_rows = {H_SLAB: pooled_sum.rearrange("c (a w) -> c a w", a=4)}
@@ -69,6 +73,7 @@ def tile_hypernetfullyconnectedflexilayersizearch_pa_k_kernel(
         factor = {}
         codes = {}
         planes = {}
+        raw = {}
         banks = {}
         grouped = {}
         product = {}
@@ -139,7 +144,7 @@ def tile_hypernetfullyconnectedflexilayersizearch_pa_k_kernel(
         factor[H_SLAB] = per_count[:]
 
         def square(s, bank, n, total):
-            squares = scratch.tile([P, SLAB], BF16, name="squares")
+            squares = unread.tile([P, SLAB // 2], BF16, name="squares")
             nc.scalar.activation(
                 out=squares[:, 0 : n * BANK_VALUES],
                 in_=slab_tile[s][:, bank * BANK_VALUES : (bank + n) * BANK_VALUES],
@@ -169,6 +174,7 @@ def tile_hypernetfullyconnectedflexilayersizearch_pa_k_kernel(
                     )
             one_over_length(factor[s], factor[s] if len(pieces) > 1 else sums[:, 0:1])
 
+        gram_sums = const.tile([P, 2], F32)
         v1_sums = const.tile([P, V1_ROWS], F32)
         factor[V1_SLAB] = const.tile([P, V1_ROWS], F32, name="v1_factor")[:]
 
@@ -178,22 +184,28 @@ def tile_hypernetfullyconnectedflexilayersizearch_pa_k_kernel(
             cols = slice(first, first + n)
             one_over_length(factor[V1_SLAB][:, cols], v1_sums[:, cols])
 
-        def fetch_slab(s):
-            new_slab(s)
-            for bank in range(0, SLAB_BANKS, 4):
-                fetch(s, bank, 4)
-
         def prepare(s):
             if s == 2:
                 v0_factors(s, (2, 2, 4))
                 return
-            fetch_slab(s)
+            if s == GRAM_SLAB:
+                square(s, GRAM_BANKS, SLAB_BANKS - GRAM_BANKS, gram_sums[:, 1:2])
+                return
+            new_slab(s)
+            if s == 3:
+                new_slab(GRAM_SLAB)
+                fetch(GRAM_SLAB, 0, 2)
+            for bank in range(0, SLAB_BANKS, 4):
+                fetch(s, bank, 4)
+            if s == 3:
+                fetch(GRAM_SLAB, 2, 2)
+                fetch(GRAM_SLAB, 4, 4)
             if s == V1_SLAB:
                 nc.sync.dma_start(out=b1_all[:], in_=b1.partition_broadcast(P))
                 v1_factors(0, 4)
                 v1_factors(4, 4)
             else:
-                v0_factors(s, (8,))
+                v0_factors(s, (4, 4))
 
         def scale(m):
             s, b, n = UNITS[m]
@@ -228,6 +240,48 @@ def tile_hypernetfullyconnectedflexilayersizearch_pa_k_kernel(
                         xt[:, i, :], words[:, block * P : (block + 1) * P], ident[:]
                     )
                 banks[m].append(xt)
+
+        def gram_transposes(b):
+            words = slab_tile[GRAM_SLAB][:].bitcast(F32)
+            raw[b] = psum_t.tile([P, BANK_BLOCKS, P], F32, tag="xt", name="raw_bank")
+            for i in range(BANK_BLOCKS):
+                block = BANK_BLOCKS * b + i
+                nc.tensor.transpose(raw[b][:, i, :], words[:, block * P : (block + 1) * P], ident[:])
+
+        def gram_copy(b):
+            words = scratch.tile([P, BANK_BLOCKS * P], F32, name="raw_words")
+            nc.vector.tensor_copy(out=words[:], in_=raw[b][:].rearrange("p i r -> p (i r)"))
+            raw[b] = words
+
+        def gram_multiply(b):
+            pairs = raw[b][:].bitcast(BF16).rearrange("p (i r e) -> p i r e", r=P, e=2)
+            for i in range(BANK_BLOCKS):
+                for e in range(2):
+                    values = pairs[:, i, :, e]
+                    nc.tensor.matmul(
+                        gram[0][:],
+                        lhsT=values,
+                        rhs=values,
+                        start=(b == 0 and i == 0 and e == 0),
+                        stop=(b == GRAM_BANKS - 1 and i == BANK_BLOCKS - 1 and e == 1),
+                    )
+
+        def gram_factors():
+            diagonal = scratch.tile([P, P], F32, name="diagonal")
+            nc.vector.scalar_tensor_tensor(
+                out=diagonal[:],
+                in0=gram[0][:],
+                scalar=1.0,
+                in1=ident[:],
+                op0=ALU.mult,
+                op1=ALU.mult,
+                accum_out=gram_sums[:, 0:1],
+            )
+            factor[GRAM_SLAB] = stats.tile([P, 1], F32, name="factor")[:]
+            nc.gpsimd.tensor_tensor(
+                out=factor[GRAM_SLAB], in0=gram_sums[:, 0:1], in1=gram_sums[:, 1:2], op=ALU.add
+            )
+            one_over_length(factor[GRAM_SLAB], factor[GRAM_SLAB])
 
         def empty_banks(m):
             n = UNITS[m][2]
@@ -269,7 +323,9 @@ def tile_hypernetfullyconnectedflexilayersizearch_pa_k_kernel(
             s, first, banks_here = UNITS[m]
             if 1 <= s <= V0_SLABS:
                 if first == 0 and (s - 1) % BANK_BLOCKS == 0:
-                    acc = psum_acc.tile([P, BANK_BLOCKS, P], F32, name="acc")
+                    acc = psum_acc.tile(
+                        [P, BANK_BLOCKS, P], F32, tag="acc%d" % ((s - 1) // BANK_BLOCKS), name="acc"
+                    )
                     for q in range(BANK_BLOCKS):
                         product[s + q] = acc[:, q, :]
                 for n in range(BANK_PASSES * first, BANK_PASSES * (first + banks_here)):
@@ -337,8 +393,14 @@ def tile_hypernetfullyconnectedflexilayersizearch_pa_k_kernel(
         scale(0)
         transposes(0)
         scaled = 0
+        gram = []
         for m, (s, first, n) in enumerate(UNITS):
             empty_banks(m)
+            bank = m - GRAM_FROM
+            if 1 <= bank <= GRAM_BANKS:
+                gram_copy(bank - 1)
+            if bank == GRAM_BANKS + 1:
+                gram_factors()
             ahead = 2 if m + 2 >= SCALAR_FROM else 1
             while scaled < min(m + ahead, LAST):
                 scaled += 1
@@ -354,10 +416,18 @@ def tile_hypernetfullyconnectedflexilayersizearch_pa_k_kernel(
                 nc.tensor.transpose(vec_t[:], vec_rows[:], ident[:])
             if m == 2:
                 nc.vector.tensor_copy(out=vecs[:], in_=vec_t[:, 0:12].bitcast(BF16))
-            if first == 0 and s + LEAD <= V1_SLAB:
+            if first == 0 and s + LEAD <= V0_SLABS:
                 prepare(s + LEAD)
+                if s + LEAD == V0_SLABS:
+                    prepare(V1_SLAB)
             if m == V1_FIRST:
                 group_hidden(0)
+            if bank == 0:
+                gram.append(psum_acc.tile([P, P], F32, tag="acc1", name="gram"))
+            if 0 <= bank < GRAM_BANKS:
+                gram_transposes(bank)
+            if 1 <= bank <= GRAM_BANKS:
+                gram_multiply(bank - 1)
             quantise(m)
             if m == V1_FIRST:
                 group_hidden(1)

@@ -291,7 +291,7 @@ def tile_hypernetfullyconnectedflexilayersizearch_pa_k_kernel(
             for b, xt in enumerate(banks[m]):
                 target = grouped[m][:, BANK_PASSES * b : BANK_PASSES * (b + 1), :, :]
                 planes_uv = xt[:].rearrange("p (n u) r -> p n r u", u=2)
-                if m > SCALAR_FROM or (m == SCALAR_FROM and b >= n // 2):
+                if m >= SCALAR_FROM:
                     nc.scalar.copy(out=target, in_=planes_uv)
                 else:
                     nc.vector.tensor_copy(out=target, in_=planes_uv)
@@ -307,12 +307,15 @@ def tile_hypernetfullyconnectedflexilayersizearch_pa_k_kernel(
                 planes[s] = pool.tile(
                     [P, SLAB_PASSES, P], U8, name=label + "_planes", align_bytes=64
                 )
-            passes = slice(BANK_PASSES * first, BANK_PASSES * (first + n))
-            nc.vector.quantize_mx(
-                out=codes[s][:, passes, :].rearrange("p n r -> p (n r)").bitcast(FP8X4),
-                scales=planes[s][:, passes, :].rearrange("p n r -> p (n r)"),
-                in_=grouped[m][:].rearrange("p n r u -> p (n r u)").bitcast(BF16),
-            )
+            step = 1 if m == LAST else n
+            for b in range(0, n, step):
+                passes = slice(BANK_PASSES * (first + b), BANK_PASSES * (first + b + step))
+                words = grouped[m][:, BANK_PASSES * b : BANK_PASSES * (b + step), :, :]
+                nc.vector.quantize_mx(
+                    out=codes[s][:, passes, :].rearrange("p n r -> p (n r)").bitcast(FP8X4),
+                    scales=planes[s][:, passes, :].rearrange("p n r -> p (n r)"),
+                    in_=words.rearrange("p n r u -> p (n r u)").bitcast(BF16),
+                )
 
         a0_rows = const.tile([P, V0_SLABS, P], BF16)
         a0_grouped = const.tile([P, L1_PASSES, P, 4], BF16, align_bytes=64)

@@ -42,7 +42,9 @@ LAST = len(UNITS) - 1
 GRAM_SLAB = 6
 GRAM_BANKS = SLAB_BANKS - 1
 GRAM_FROM = UNITS.index((1, 0, 4))
-SCALAR_FROM = V1_FIRST - 4
+SHARE_FROM = UNITS.index((5, 4, 4))
+SHARE = 2
+SQUARES_FIRST = 6
 
 FLOPS = 2 * P * D_IN * HIDDEN + 2 * P * HIDDEN * HIDDEN
 
@@ -70,6 +72,7 @@ def tile_hypernetfullyconnectedflexilayersizearch_pa_k_kernel(
         dram_rows[V1_SLAB] = V1.rearrange("(a p e) k -> p a (e k)", p=P, e=2)
 
         slab_tile = {}
+        sums = {}
         factor = {}
         codes = {}
         planes = {}
@@ -158,37 +161,54 @@ def tile_hypernetfullyconnectedflexilayersizearch_pa_k_kernel(
                 out=result, in0=lengths, in1=minus_half[:, 0:width], op=ALU.pow
             )
 
-        def v0_factors(s, pieces):
-            sums = stats.tile([P, SLAB_BANKS], F32, name="sums")
-            factor[s] = stats.tile([P, 1], F32, name="factor")[:]
+        def v0_squares(s, pieces):
+            sums[s] = stats.tile([P, SLAB_BANKS], F32, name="sums")[:, 0 : len(pieces)]
             bank = 0
             for i, n in enumerate(pieces):
-                square(s, bank, n, sums[:, i : i + 1])
+                square(s, bank, n, sums[s][:, i : i + 1])
                 bank += n
-                if i > 0:
-                    nc.gpsimd.tensor_tensor(
-                        out=factor[s],
-                        in0=sums[:, 0:1] if i == 1 else factor[s],
-                        in1=sums[:, i : i + 1],
-                        op=ALU.add,
-                    )
-            one_over_length(factor[s], factor[s] if len(pieces) > 1 else sums[:, 0:1])
+
+        def v0_factors(s):
+            factor[s] = stats.tile([P, 1], F32, name="factor")[:]
+            total = sums[s][:, 0:1]
+            for i in range(1, sums[s].shape[1]):
+                nc.gpsimd.tensor_tensor(
+                    out=factor[s], in0=total, in1=sums[s][:, i : i + 1], op=ALU.add
+                )
+                total = factor[s]
+            one_over_length(factor[s], total)
 
         gram_sums = const.tile([P, 2], F32)
         v1_sums = const.tile([P, V1_ROWS], F32)
         factor[V1_SLAB] = const.tile([P, V1_ROWS], F32, name="v1_factor")[:]
 
-        def v1_factors(first, n):
-            for bank in range(first, first + n):
-                square(V1_SLAB, bank, 1, v1_sums[:, bank : bank + 1])
-            cols = slice(first, first + n)
+        def pair_squares(s, pair):
+            bank = 2 * pair
+            if s == V1_SLAB:
+                for b in (bank, bank + 1):
+                    square(s, b, 1, v1_sums[:, b : b + 1])
+                return
+            if pair == 0:
+                sums[s] = stats.tile([P, SLAB_BANKS], F32, name="sums")[:, 0 : SLAB_BANKS // 2]
+            square(s, bank, 2, sums[s][:, pair : pair + 1])
+
+        def v1_factors(first):
+            cols = slice(first, first + 4)
             one_over_length(factor[V1_SLAB][:, cols], v1_sums[:, cols])
+
+        def need_factors(m):
+            s, first, n = UNITS[m]
+            if s not in factor:
+                v0_factors(s)
+            if s == V1_SLAB and first % 4 == 0:
+                v1_factors(first)
 
         def prepare(s):
             if s == 2:
-                v0_factors(s, (2, 2, 4))
+                v0_squares(s, (2, 2, 4))
                 return
             if s == GRAM_SLAB:
+                sums[s] = gram_sums[:]
                 square(s, GRAM_BANKS, SLAB_BANKS - GRAM_BANKS, gram_sums[:, 1:2])
                 return
             new_slab(s)
@@ -202,16 +222,16 @@ def tile_hypernetfullyconnectedflexilayersizearch_pa_k_kernel(
                 fetch(GRAM_SLAB, 4, 4)
             if s == V1_SLAB:
                 nc.sync.dma_start(out=b1_all[:], in_=b1.partition_broadcast(P))
-                v1_factors(0, 4)
-                v1_factors(4, 4)
-            else:
-                v0_factors(s, (4, 4))
+            elif s <= GRAM_SLAB:
+                v0_squares(s, (4, 4))
 
         def scale(m):
+            need_factors(m)
             s, b, n = UNITS[m]
+            end = (b + n) * BANK_VALUES
             span = SLAB // factor[s].shape[1]
-            piece = min(span, BANK_VALUES if m == 0 else n * BANK_VALUES)
-            for start in range(b * BANK_VALUES, (b + n) * BANK_VALUES, piece):
+            piece = BANK_VALUES if m == 0 else min(span, end - b * BANK_VALUES)
+            for start in range(b * BANK_VALUES, end, piece):
                 values = slab_tile[s][:, start : start + piece]
                 row = slice(start // span, start // span + 1)
                 if s == H_SLAB:
@@ -266,7 +286,7 @@ def tile_hypernetfullyconnectedflexilayersizearch_pa_k_kernel(
                         stop=(b == GRAM_BANKS - 1 and i == BANK_BLOCKS - 1 and e == 1),
                     )
 
-        def gram_factors():
+        def gram_diagonal():
             diagonal = scratch.tile([P, P], F32, name="diagonal")
             nc.vector.scalar_tensor_tensor(
                 out=diagonal[:],
@@ -277,11 +297,6 @@ def tile_hypernetfullyconnectedflexilayersizearch_pa_k_kernel(
                 op1=ALU.mult,
                 accum_out=gram_sums[:, 0:1],
             )
-            factor[GRAM_SLAB] = stats.tile([P, 1], F32, name="factor")[:]
-            nc.gpsimd.tensor_tensor(
-                out=factor[GRAM_SLAB], in0=gram_sums[:, 0:1], in1=gram_sums[:, 1:2], op=ALU.add
-            )
-            one_over_length(factor[GRAM_SLAB], factor[GRAM_SLAB])
 
         def empty_banks(m):
             n = UNITS[m][2]
@@ -291,7 +306,7 @@ def tile_hypernetfullyconnectedflexilayersizearch_pa_k_kernel(
             for b, xt in enumerate(banks[m]):
                 target = grouped[m][:, BANK_PASSES * b : BANK_PASSES * (b + 1), :, :]
                 planes_uv = xt[:].rearrange("p (n u) r -> p n r u", u=2)
-                if m >= SCALAR_FROM:
+                if m >= V1_FIRST or (m >= SHARE_FROM and b >= n - SHARE):
                     nc.scalar.copy(out=target, in_=planes_uv)
                 else:
                     nc.vector.tensor_copy(out=target, in_=planes_uv)
@@ -397,14 +412,15 @@ def tile_hypernetfullyconnectedflexilayersizearch_pa_k_kernel(
         transposes(0)
         scaled = 0
         gram = []
+        pairs = [(s, pair) for s in range(GRAM_SLAB + 1, SLABS) for pair in range(SLAB_BANKS // 2)]
         for m, (s, first, n) in enumerate(UNITS):
             empty_banks(m)
             bank = m - GRAM_FROM
             if 1 <= bank <= GRAM_BANKS:
                 gram_copy(bank - 1)
             if bank == GRAM_BANKS + 1:
-                gram_factors()
-            ahead = 2 if m + 2 >= SCALAR_FROM else 1
+                gram_diagonal()
+            ahead = 2 if m + 2 >= V1_FIRST else 1
             while scaled < min(m + ahead, LAST):
                 scaled += 1
                 scale(scaled)
@@ -413,16 +429,19 @@ def tile_hypernetfullyconnectedflexilayersizearch_pa_k_kernel(
                 for done in range(1, V0_SLABS + 1):
                     hidden_silu(done)
             if m == 0:
-                v0_factors(1, (1,) * SLAB_BANKS)
+                v0_squares(1, (1,) * SLAB_BANKS)
             if m == 1:
                 vec_t = psum_t.tile([P, P], F32, tag="xt")
                 nc.tensor.transpose(vec_t[:], vec_rows[:], ident[:])
             if m == 2:
                 nc.vector.tensor_copy(out=vecs[:], in_=vec_t[:, 0:12].bitcast(BF16))
-            if first == 0 and s + LEAD <= V0_SLABS:
+            if first == 0 and s + LEAD <= GRAM_SLAB:
                 prepare(s + LEAD)
-                if s + LEAD == V0_SLABS:
-                    prepare(V1_SLAB)
+            if first == 0 and GRAM_SLAB < s + 4 <= V1_SLAB:
+                prepare(s + 4)
+            due = SQUARES_FIRST + m - SHARE_FROM + 1 if m >= SHARE_FROM - 1 else 0
+            while pairs and len(pairs) > 12 - due:
+                pair_squares(*pairs.pop(0))
             if m == V1_FIRST:
                 group_hidden(0)
             if bank == 0:

@@ -44,7 +44,7 @@ GRAM_BANKS = SLAB_BANKS - 1
 GRAM_FROM = UNITS.index((1, 0, 4))
 SHARE_FROM = UNITS.index((5, 4, 4))
 SHARE = 2
-SQUARES_FIRST = 6
+SQUARES_FIRST = 2
 
 FLOPS = 2 * P * D_IN * HIDDEN + 2 * P * HIDDEN * HIDDEN
 
@@ -109,10 +109,19 @@ def tile_hypernetfullyconnectedflexilayersizearch_pa_k_kernel(
         fetch(H_SLAB, 0, 1)
         fetch(1, 0, 1)
         fetch(H_SLAB, 1, 1)
+        fetch(H_SLAB, 2, 1)
         fetch(1, 1, 1)
+        fetch(H_SLAB, 3, 1)
         fetch(1, 2, 1)
-        fetch(H_SLAB, 2, 2)
+        fetch(H_SLAB, 4, 1)
         fetch(1, 3, 1)
+        fetch(H_SLAB, 5, 1)
+        fetch(1, 4, 1)
+        fetch(H_SLAB, 6, 1)
+        fetch(1, 5, 1)
+        fetch(H_SLAB, 7, 1)
+        fetch(1, 6, 1)
+        fetch(1, 7, 1)
         vec_rows = const.tile([P, P], F32)
         nc.vector.memset(vec_rows[:], 0.0)
         for n, vec in enumerate((g0, b0, g1)):
@@ -120,13 +129,6 @@ def tile_hypernetfullyconnectedflexilayersizearch_pa_k_kernel(
                 out=vec_rows[:].bitcast(BF16)[4 * n : 4 * n + 4, :],
                 in_=vec.rearrange("(r w) -> r w", r=4),
             )
-
-        fetch(1, 4, 1)
-        fetch(H_SLAB, 4, 2)
-        fetch(1, 5, 1)
-        fetch(1, 6, 1)
-        fetch(H_SLAB, 6, 2)
-        fetch(1, 7, 1)
         fetch(2, 0, 2)
         fetch(2, 2, 2)
         fetch(2, 4, 4)
@@ -219,10 +221,11 @@ def tile_hypernetfullyconnectedflexilayersizearch_pa_k_kernel(
                 fetch(s, bank, 4)
             if s == 3:
                 fetch(GRAM_SLAB, 2, 2)
+            if s == 4:
                 fetch(GRAM_SLAB, 4, 4)
             if s == V1_SLAB:
                 nc.sync.dma_start(out=b1_all[:], in_=b1.partition_broadcast(P))
-            elif s <= GRAM_SLAB:
+            elif s < V0_SLABS:
                 v0_squares(s, (4, 4))
 
         def scale(m):
@@ -230,7 +233,7 @@ def tile_hypernetfullyconnectedflexilayersizearch_pa_k_kernel(
             s, b, n = UNITS[m]
             end = (b + n) * BANK_VALUES
             span = SLAB // factor[s].shape[1]
-            piece = BANK_VALUES if m == 0 else min(span, end - b * BANK_VALUES)
+            piece = BANK_VALUES if s == H_SLAB else min(span, end - b * BANK_VALUES)
             for start in range(b * BANK_VALUES, end, piece):
                 values = slab_tile[s][:, start : start + piece]
                 row = slice(start // span, start // span + 1)
@@ -412,7 +415,7 @@ def tile_hypernetfullyconnectedflexilayersizearch_pa_k_kernel(
         transposes(0)
         scaled = 0
         gram = []
-        pairs = [(s, pair) for s in range(GRAM_SLAB + 1, SLABS) for pair in range(SLAB_BANKS // 2)]
+        pairs = [(s, pair) for s in range(V0_SLABS, SLABS) for pair in range(SLAB_BANKS // 2)]
         for m, (s, first, n) in enumerate(UNITS):
             empty_banks(m)
             bank = m - GRAM_FROM
@@ -420,6 +423,8 @@ def tile_hypernetfullyconnectedflexilayersizearch_pa_k_kernel(
                 gram_copy(bank - 1)
             if bank == GRAM_BANKS + 1:
                 gram_diagonal()
+            if m == 3:
+                nc.vector.tensor_copy(out=vecs[:], in_=vec_t[:, 0:12].bitcast(BF16))
             ahead = 2 if m + 2 >= V1_FIRST else 1
             while scaled < min(m + ahead, LAST):
                 scaled += 1
@@ -430,17 +435,15 @@ def tile_hypernetfullyconnectedflexilayersizearch_pa_k_kernel(
                     hidden_silu(done)
             if m == 0:
                 v0_squares(1, (1,) * SLAB_BANKS)
-            if m == 1:
+            if m == 2:
                 vec_t = psum_t.tile([P, P], F32, tag="xt")
                 nc.tensor.transpose(vec_t[:], vec_rows[:], ident[:])
-            if m == 2:
-                nc.vector.tensor_copy(out=vecs[:], in_=vec_t[:, 0:12].bitcast(BF16))
             if first == 0 and s + LEAD <= GRAM_SLAB:
                 prepare(s + LEAD)
             if first == 0 and GRAM_SLAB < s + 4 <= V1_SLAB:
                 prepare(s + 4)
             due = SQUARES_FIRST + m - SHARE_FROM + 1 if m >= SHARE_FROM - 1 else 0
-            while pairs and len(pairs) > 12 - due:
+            while pairs and len(pairs) > 8 - due:
                 pair_squares(*pairs.pop(0))
             if m == V1_FIRST:
                 group_hidden(0)

@@ -16,6 +16,7 @@ D_IN = 8192
 HIDDEN = 1024
 K_PASS = 512
 BANK = 512
+PSUM_BANKS = 8
 
 SLAB = 8192
 BANK_VALUES = 2 * BANK
@@ -42,9 +43,15 @@ LAST = len(UNITS) - 1
 GRAM_SLAB = 6
 GRAM_BANKS = SLAB_BANKS - 1
 GRAM_FROM = UNITS.index((1, 0, 4))
-SHARE_FROM = UNITS.index((5, 4, 4))
+POOL_SLAB = 7
+POOL_PIECE = 6 * P
+POOL_UNITS = [UNITS.index((s, b, 4)) for s, b in ((2, 0), (3, 0), (3, 4), (4, 0), (4, 4))]
+POOL_VALUES = len(POOL_UNITS) * POOL_PIECE
+POOL_DONE = POOL_UNITS[-1] + 1
+UNREAD = max(SLAB // 2, SLAB - POOL_VALUES)
+SHARE_FROM = UNITS.index((5, 0, 4))
 SHARE = 2
-SQUARES_FIRST = 2
+SQUARES_FIRST = 1
 
 FLOPS = 2 * P * D_IN * HIDDEN + 2 * P * HIDDEN * HIDDEN
 
@@ -62,8 +69,8 @@ def tile_hypernetfullyconnectedflexilayersizearch_pa_k_kernel(
         regroup = ctx.enter_context(tc.tile_pool(name="regroup", bufs=3))
         weights = ctx.enter_context(tc.tile_pool(name="weights", bufs=2))
         final = ctx.enter_context(tc.tile_pool(name="final", bufs=3))
-        psum_t = ctx.enter_context(tc.psum_pool(name="psum_t", bufs=6))
-        psum_acc = ctx.enter_context(tc.psum_pool(name="psum_acc", bufs=1))
+        psum = ctx.enter_context(tc.psum_pool(name="psum", bufs=1))
+        powers = ctx.enter_context(tc.tile_pool(name="powers", bufs=2))
         ctx.enter_context(tc.manual_schedule())
         v0_rows = V0.rearrange("(i2 p e) (a w) -> i2 e p a w", p=P, e=2, a=4)
         dram_rows = {H_SLAB: pooled_sum.rearrange("c (a w) -> c a w", a=4)}
@@ -79,7 +86,27 @@ def tile_hypernetfullyconnectedflexilayersizearch_pa_k_kernel(
         raw = {}
         banks = {}
         grouped = {}
+        awaited = const.tile([P, 1], BF16)
+        last_codes = [None]
+        pool_acc = []
         product = {}
+
+        ring = list(range(PSUM_BANKS))
+        held = {}
+
+        def bank_tile(number):
+            return psum.tile([P, BANK_BLOCKS, P], F32, tag="bank%d" % number, name="bank")
+
+        def next_bank():
+            ring.append(ring.pop(0))
+            return bank_tile(ring[-1])
+
+        def hold_bank(user):
+            held[user] = ring.pop(0)
+            return bank_tile(held[user])
+
+        def put_back(user):
+            ring.append(held[user])
 
         def new_slab(s):
             slab_tile[s] = slabs.tile([P, SLAB], BF16, name="slab")
@@ -98,14 +125,21 @@ def tile_hypernetfullyconnectedflexilayersizearch_pa_k_kernel(
 
         minus_half = const.tile([P, V1_ROWS], F32)
         nc.vector.memset(minus_half[:], -0.5)
+        cnt = const.tile([P, 1], BF16)
+        nc.scalar.dma_start(out=cnt[:], in_=count)
         table_load = const.tile([P, 1], F32)
         nc.scalar.activation(out=table_load[:], in_=minus_half[:, 0:1], func=ACT.Silu)
+        vec_rows = const.tile([P, P], F32)
+        nc.vector.memset(vec_rows[:], 0.0)
+        for n, vec in enumerate((g0, b0, g1)):
+            nc.scalar.dma_start(
+                out=vec_rows[:].bitcast(BF16)[4 * n : 4 * n + 4, :],
+                in_=vec.rearrange("(r w) -> r w", r=4),
+            )
 
-        for s in (1, H_SLAB, 2):
+        for s in (H_SLAB, 1, 2):
             new_slab(s)
 
-        cnt = const.tile([P, 1], BF16)
-        nc.sync.dma_start(out=cnt[:], in_=count)
         fetch(H_SLAB, 0, 1)
         fetch(1, 0, 1)
         fetch(H_SLAB, 1, 1)
@@ -122,13 +156,6 @@ def tile_hypernetfullyconnectedflexilayersizearch_pa_k_kernel(
         fetch(H_SLAB, 7, 1)
         fetch(1, 6, 1)
         fetch(1, 7, 1)
-        vec_rows = const.tile([P, P], F32)
-        nc.vector.memset(vec_rows[:], 0.0)
-        for n, vec in enumerate((g0, b0, g1)):
-            nc.sync.dma_start(
-                out=vec_rows[:].bitcast(BF16)[4 * n : 4 * n + 4, :],
-                in_=vec.rearrange("(r w) -> r w", r=4),
-            )
         fetch(2, 0, 2)
         fetch(2, 2, 2)
         fetch(2, 4, 4)
@@ -149,7 +176,7 @@ def tile_hypernetfullyconnectedflexilayersizearch_pa_k_kernel(
         factor[H_SLAB] = per_count[:]
 
         def square(s, bank, n, total):
-            squares = unread.tile([P, SLAB // 2], BF16, name="squares")
+            squares = unread.tile([P, UNREAD], BF16, name="squares")
             nc.scalar.activation(
                 out=squares[:, 0 : n * BANK_VALUES],
                 in_=slab_tile[s][:, bank * BANK_VALUES : (bank + n) * BANK_VALUES],
@@ -181,6 +208,9 @@ def tile_hypernetfullyconnectedflexilayersizearch_pa_k_kernel(
             one_over_length(factor[s], total)
 
         gram_sums = const.tile([P, 2], F32)
+        pool_sums = const.tile([P, 2], F32)
+        ones = const.tile([P, 2], F32)
+        nc.vector.memset(ones[:], 1.0)
         v1_sums = const.tile([P, V1_ROWS], F32)
         factor[V1_SLAB] = const.tile([P, V1_ROWS], F32, name="v1_factor")[:]
 
@@ -213,19 +243,29 @@ def tile_hypernetfullyconnectedflexilayersizearch_pa_k_kernel(
                 sums[s] = gram_sums[:]
                 square(s, GRAM_BANKS, SLAB_BANKS - GRAM_BANKS, gram_sums[:, 1:2])
                 return
+            if s == POOL_SLAB:
+                sums[s] = pool_sums[:]
+                squares = unread.tile([P, UNREAD], BF16, name="squares")
+                nc.scalar.activation(
+                    out=squares[:, 0 : SLAB - POOL_VALUES],
+                    in_=slab_tile[s][:, POOL_VALUES:SLAB],
+                    func=ACT.Square,
+                    accum_out=pool_sums[:, 1:2],
+                )
+                return
             new_slab(s)
             if s == 3:
-                new_slab(GRAM_SLAB)
-                fetch(GRAM_SLAB, 0, 2)
+                for early in (GRAM_SLAB, POOL_SLAB):
+                    new_slab(early)
+                    fetch(early, 0, 2)
             for bank in range(0, SLAB_BANKS, 4):
                 fetch(s, bank, 4)
-            if s == 3:
-                fetch(GRAM_SLAB, 2, 2)
-            if s == 4:
-                fetch(GRAM_SLAB, 4, 4)
+            if s in (3, 4):
+                for early in (GRAM_SLAB, POOL_SLAB):
+                    fetch(early, 2 if s == 3 else 4, 2 if s == 3 else 4)
             if s == V1_SLAB:
                 nc.sync.dma_start(out=b1_all[:], in_=b1.partition_broadcast(P))
-            elif s < V0_SLABS:
+            elif s < GRAM_SLAB:
                 v0_squares(s, (4, 4))
 
         def scale(m):
@@ -256,7 +296,7 @@ def tile_hypernetfullyconnectedflexilayersizearch_pa_k_kernel(
             words = slab_tile[s][:].bitcast(F32)
             banks[m] = []
             for b in range(first, first + n):
-                xt = psum_t.tile([P, BANK_BLOCKS, P], F32, name="xt")
+                xt = next_bank()
                 for i in range(BANK_BLOCKS):
                     block = BANK_BLOCKS * b + i
                     nc.tensor.transpose(
@@ -264,9 +304,34 @@ def tile_hypernetfullyconnectedflexilayersizearch_pa_k_kernel(
                     )
                 banks[m].append(xt)
 
+        def pool_squares(step):
+            nc.gpsimd.tensor_copy(out=awaited[:], in_=last_codes[0])
+            values = slab_tile[POOL_SLAB][:, step * POOL_PIECE : (step + 1) * POOL_PIECE]
+            powers_tile = powers.tile([P, POOL_PIECE], F32, name="powers")
+            nc.gpsimd.tensor_tensor(out=powers_tile[:], in0=values, in1=values, op=ALU.mult)
+            return powers_tile
+
+        def pool_add(step, powers_tile):
+            for i in range(POOL_PIECE // P):
+                nc.tensor.matmul(
+                    pool_acc[0][:, 0, :],
+                    lhsT=powers_tile[:, i * P : (i + 1) * P],
+                    rhs=ident[:],
+                    is_transpose=True,
+                    start=(step == 0 and i == 0),
+                    stop=(step == len(POOL_UNITS) - 1 and i == POOL_PIECE // P - 1),
+                )
+
+        def pool_total():
+            part = scratch.tile([P, P], F32, name="pool_part")
+            nc.vector.tensor_copy(out=part[:], in_=pool_acc[0][:, 0, :])
+            nc.tensor.matmul(
+                pool_acc[0][:, 1, 0:2], lhsT=part[:], rhs=ones[:], start=True, stop=True
+            )
+
         def gram_transposes(b):
             words = slab_tile[GRAM_SLAB][:].bitcast(F32)
-            raw[b] = psum_t.tile([P, BANK_BLOCKS, P], F32, tag="xt", name="raw_bank")
+            raw[b] = next_bank()
             for i in range(BANK_BLOCKS):
                 block = BANK_BLOCKS * b + i
                 nc.tensor.transpose(raw[b][:, i, :], words[:, block * P : (block + 1) * P], ident[:])
@@ -282,7 +347,7 @@ def tile_hypernetfullyconnectedflexilayersizearch_pa_k_kernel(
                 for e in range(2):
                     values = pairs[:, i, :, e]
                     nc.tensor.matmul(
-                        gram[0][:],
+                        gram[0][:, 0, :],
                         lhsT=values,
                         rhs=values,
                         start=(b == 0 and i == 0 and e == 0),
@@ -293,7 +358,7 @@ def tile_hypernetfullyconnectedflexilayersizearch_pa_k_kernel(
             diagonal = scratch.tile([P, P], F32, name="diagonal")
             nc.vector.scalar_tensor_tensor(
                 out=diagonal[:],
-                in0=gram[0][:],
+                in0=gram[0][:, 0, :],
                 scalar=1.0,
                 in1=ident[:],
                 op0=ALU.mult,
@@ -309,7 +374,7 @@ def tile_hypernetfullyconnectedflexilayersizearch_pa_k_kernel(
             for b, xt in enumerate(banks[m]):
                 target = grouped[m][:, BANK_PASSES * b : BANK_PASSES * (b + 1), :, :]
                 planes_uv = xt[:].rearrange("p (n u) r -> p n r u", u=2)
-                if m >= V1_FIRST or (m >= SHARE_FROM and b >= n - SHARE):
+                if m >= V1_FIRST or (m >= SHARE_FROM and b >= n - (3 if (m - SHARE_FROM) % 4 == 1 else SHARE)):
                     nc.scalar.copy(out=target, in_=planes_uv)
                 else:
                     nc.vector.tensor_copy(out=target, in_=planes_uv)
@@ -329,6 +394,9 @@ def tile_hypernetfullyconnectedflexilayersizearch_pa_k_kernel(
             for b in range(0, n, step):
                 passes = slice(BANK_PASSES * (first + b), BANK_PASSES * (first + b + step))
                 words = grouped[m][:, BANK_PASSES * b : BANK_PASSES * (b + step), :, :]
+                last_codes[0] = codes[s][:, passes, :].rearrange("p n r -> p (n r)").bitcast(BF16)[
+                    :, 0:1
+                ]
                 nc.vector.quantize_mx(
                     out=codes[s][:, passes, :].rearrange("p n r -> p (n r)").bitcast(FP8X4),
                     scales=planes[s][:, passes, :].rearrange("p n r -> p (n r)"),
@@ -344,9 +412,7 @@ def tile_hypernetfullyconnectedflexilayersizearch_pa_k_kernel(
             s, first, banks_here = UNITS[m]
             if 1 <= s <= V0_SLABS:
                 if first == 0 and (s - 1) % BANK_BLOCKS == 0:
-                    acc = psum_acc.tile(
-                        [P, BANK_BLOCKS, P], F32, tag="acc%d" % ((s - 1) // BANK_BLOCKS), name="acc"
-                    )
+                    acc = hold_bank(("products", s))
                     for q in range(BANK_BLOCKS):
                         product[s + q] = acc[:, q, :]
                 for n in range(BANK_PASSES * first, BANK_PASSES * (first + banks_here)):
@@ -360,7 +426,7 @@ def tile_hypernetfullyconnectedflexilayersizearch_pa_k_kernel(
                         stop=(n == SLAB_PASSES - 1),
                     )
             if s == V1_SLAB:
-                product[m] = psum_t.tile([P, BANK], F32, tag="xt", name="out_bank")
+                product[m] = next_bank()[:].rearrange("p i r -> p (i r)")
                 for i in range(first, first + banks_here):
                     cols = slice((i - first) * P, (i - first + 1) * P)
                     for n in range(L1_PASSES):
@@ -417,14 +483,23 @@ def tile_hypernetfullyconnectedflexilayersizearch_pa_k_kernel(
         gram = []
         pairs = [(s, pair) for s in range(V0_SLABS, SLABS) for pair in range(SLAB_BANKS // 2)]
         for m, (s, first, n) in enumerate(UNITS):
+            if m in POOL_UNITS:
+                need_factors(m + 1)
+                powers_tile = pool_squares(POOL_UNITS.index(m))
             empty_banks(m)
+            if m == POOL_DONE + 1:
+                pool_total()
+            if m == POOL_DONE + 2:
+                nc.vector.tensor_copy(out=pool_sums[:, 0:1], in_=pool_acc[0][:, 1, 0:1])
+                put_back("pool")
             bank = m - GRAM_FROM
             if 1 <= bank <= GRAM_BANKS:
                 gram_copy(bank - 1)
             if bank == GRAM_BANKS + 1:
                 gram_diagonal()
+                put_back("gram")
             if m == 3:
-                nc.vector.tensor_copy(out=vecs[:], in_=vec_t[:, 0:12].bitcast(BF16))
+                nc.vector.tensor_copy(out=vecs[:], in_=vec_t[:, 0, 0:12].bitcast(BF16))
             ahead = 2 if m + 2 >= V1_FIRST else 1
             while scaled < min(m + ahead, LAST):
                 scaled += 1
@@ -436,11 +511,13 @@ def tile_hypernetfullyconnectedflexilayersizearch_pa_k_kernel(
             if m == 0:
                 v0_squares(1, (1,) * SLAB_BANKS)
             if m == 2:
-                vec_t = psum_t.tile([P, P], F32, tag="xt")
-                nc.tensor.transpose(vec_t[:], vec_rows[:], ident[:])
+                vec_t = next_bank()
+                nc.tensor.transpose(vec_t[:, 0, :], vec_rows[:], ident[:])
             if first == 0 and s + LEAD <= GRAM_SLAB:
                 prepare(s + LEAD)
-            if first == 0 and GRAM_SLAB < s + 4 <= V1_SLAB:
+            if first == 0 and s + LEAD == GRAM_SLAB:
+                prepare(POOL_SLAB)
+            if first == 0 and POOL_SLAB < s + 4 <= V1_SLAB:
                 prepare(s + 4)
             due = SQUARES_FIRST + m - SHARE_FROM + 1 if m >= SHARE_FROM - 1 else 0
             while pairs and len(pairs) > 8 - due:
@@ -448,7 +525,7 @@ def tile_hypernetfullyconnectedflexilayersizearch_pa_k_kernel(
             if m == V1_FIRST:
                 group_hidden(0)
             if bank == 0:
-                gram.append(psum_acc.tile([P, P], F32, tag="acc1", name="gram"))
+                gram.append(hold_bank("gram"))
             if 0 <= bank < GRAM_BANKS:
                 gram_transposes(bank)
             if 1 <= bank <= GRAM_BANKS:
@@ -458,5 +535,9 @@ def tile_hypernetfullyconnectedflexilayersizearch_pa_k_kernel(
                 group_hidden(1)
                 quantise_hidden()
             multiply(m)
+            if m == POOL_UNITS[0]:
+                pool_acc.append(hold_bank("pool"))
+            if m in POOL_UNITS:
+                pool_add(POOL_UNITS.index(m), powers_tile)
         for m in range(V1_FIRST, LAST + 1):
             write_output(m)

@@ -51,7 +51,7 @@ POOL_DONE = POOL_UNITS[-1] + 1
 UNREAD = max(SLAB // 2, SLAB - POOL_VALUES)
 SHARE_FROM = UNITS.index((5, 0, 4))
 SHARE = 2
-SQUARES_FIRST = 1
+SQUARES_FIRST = 2
 
 FLOPS = 2 * P * D_IN * HIDDEN + 2 * P * HIDDEN * HIDDEN
 
@@ -240,11 +240,11 @@ def tile_hypernetfullyconnectedflexilayersizearch_pa_k_kernel(
                 v0_squares(s, (2, 2, 4))
                 return
             if s == GRAM_SLAB:
-                sums[s] = gram_sums[:]
+                sums[s] = gram_sums[:, 0:1]
                 square(s, GRAM_BANKS, SLAB_BANKS - GRAM_BANKS, gram_sums[:, 1:2])
                 return
             if s == POOL_SLAB:
-                sums[s] = pool_sums[:]
+                sums[s] = pool_sums[:, 0:1]
                 squares = unread.tile([P, UNREAD], BF16, name="squares")
                 nc.scalar.activation(
                     out=squares[:, 0 : SLAB - POOL_VALUES],
@@ -359,9 +359,9 @@ def tile_hypernetfullyconnectedflexilayersizearch_pa_k_kernel(
             nc.vector.scalar_tensor_tensor(
                 out=diagonal[:],
                 in0=gram[0][:, 0, :],
-                scalar=1.0,
+                scalar=gram_sums[:, 1:2],
                 in1=ident[:],
-                op0=ALU.mult,
+                op0=ALU.add,
                 op1=ALU.mult,
                 accum_out=gram_sums[:, 0:1],
             )
@@ -374,7 +374,7 @@ def tile_hypernetfullyconnectedflexilayersizearch_pa_k_kernel(
             for b, xt in enumerate(banks[m]):
                 target = grouped[m][:, BANK_PASSES * b : BANK_PASSES * (b + 1), :, :]
                 planes_uv = xt[:].rearrange("p (n u) r -> p n r u", u=2)
-                if m >= V1_FIRST or (m >= SHARE_FROM and b >= n - (3 if (m - SHARE_FROM) % 4 == 1 else SHARE)):
+                if m >= V1_FIRST or (m >= SHARE_FROM and b >= n - (3 if (m - SHARE_FROM) % 4 == 1 or m >= V1_FIRST - 2 else SHARE)):
                     nc.scalar.copy(out=target, in_=planes_uv)
                 else:
                     nc.vector.tensor_copy(out=target, in_=planes_uv)
@@ -490,7 +490,9 @@ def tile_hypernetfullyconnectedflexilayersizearch_pa_k_kernel(
             if m == POOL_DONE + 1:
                 pool_total()
             if m == POOL_DONE + 2:
-                nc.vector.tensor_copy(out=pool_sums[:, 0:1], in_=pool_acc[0][:, 1, 0:1])
+                nc.vector.tensor_scalar_add(
+                    out=pool_sums[:, 0:1], in0=pool_acc[0][:, 1, 0:1], scalar1=pool_sums[:, 1:2]
+                )
                 put_back("pool")
             bank = m - GRAM_FROM
             if 1 <= bank <= GRAM_BANKS:

@@ -48,6 +48,11 @@ POOL_PIECE = 6 * P
 POOL_UNITS = [UNITS.index((s, b, 4)) for s, b in ((2, 0), (3, 0), (3, 4), (4, 0), (4, 4))]
 POOL_VALUES = len(POOL_UNITS) * POOL_PIECE
 POOL_DONE = POOL_UNITS[-1] + 1
+EARLY_FETCHES = {
+    3: ((GRAM_SLAB, 2, 2), (POOL_SLAB, 0, 2)),
+    4: ((GRAM_SLAB, 4, 2),),
+    5: ((POOL_SLAB, 2, 2), (GRAM_SLAB, 6, 2), (POOL_SLAB, 4, 4)),
+}
 UNREAD = max(SLAB // 2, SLAB - POOL_VALUES)
 SHARE_FROM = UNITS.index((5, 0, 4))
 SHARE = 2
@@ -257,12 +262,11 @@ def tile_hypernetfullyconnectedflexilayersizearch_pa_k_kernel(
             if s == 3:
                 for early in (GRAM_SLAB, POOL_SLAB):
                     new_slab(early)
-                    fetch(early, 0, 2)
+                fetch(GRAM_SLAB, 0, 2)
             for bank in range(0, SLAB_BANKS, 4):
                 fetch(s, bank, 4)
-            if s in (3, 4):
-                for early in (GRAM_SLAB, POOL_SLAB):
-                    fetch(early, 2 if s == 3 else 4, 2 if s == 3 else 4)
+            for early, bank, n in EARLY_FETCHES.get(s, ()):
+                fetch(early, bank, n)
             if s == V1_SLAB:
                 nc.sync.dma_start(out=b1_all[:], in_=b1.partition_broadcast(P))
             elif s < GRAM_SLAB:

@@ -44,9 +44,9 @@ GRAM_SLAB = 6
 GRAM_BANKS = SLAB_BANKS - 1
 GRAM_FROM = UNITS.index((1, 0, 4))
 POOL_SLAB = 7
-POOL_PIECE = 6 * P
-POOL_UNITS = [UNITS.index((s, b, 4)) for s, b in ((2, 0), (3, 0), (3, 4), (4, 0), (4, 4))]
-POOL_VALUES = len(POOL_UNITS) * POOL_PIECE
+POOL_BLOCKS = (6, 4, 6, 4, 6, 4)
+POOL_UNITS = [UNITS.index((s, b, 4)) for s, b in ((2, 0), (2, 4), (3, 0), (3, 4), (4, 0), (4, 4))]
+POOL_VALUES = sum(POOL_BLOCKS) * P
 POOL_DONE = POOL_UNITS[-1] + 1
 EARLY_FETCHES = {
     3: ((GRAM_SLAB, 2, 2), (POOL_SLAB, 0, 2)),
@@ -56,7 +56,7 @@ EARLY_FETCHES = {
 UNREAD = max(SLAB // 2, SLAB - POOL_VALUES)
 SHARE_FROM = UNITS.index((5, 0, 4))
 SHARE = 2
-SQUARES_FIRST = 2
+LATE_PIECES = ((0, 4), (4, 2), (6, 2))
 
 FLOPS = 2 * P * D_IN * HIDDEN + 2 * P * HIDDEN * HIDDEN
 
@@ -148,20 +148,21 @@ def tile_hypernetfullyconnectedflexilayersizearch_pa_k_kernel(
         fetch(H_SLAB, 0, 1)
         fetch(1, 0, 1)
         fetch(H_SLAB, 1, 1)
-        fetch(H_SLAB, 2, 1)
         fetch(1, 1, 1)
-        fetch(H_SLAB, 3, 1)
+        fetch(H_SLAB, 2, 1)
         fetch(1, 2, 1)
-        fetch(H_SLAB, 4, 1)
+        fetch(H_SLAB, 3, 1)
         fetch(1, 3, 1)
-        fetch(H_SLAB, 5, 1)
+        fetch(H_SLAB, 4, 1)
         fetch(1, 4, 1)
-        fetch(H_SLAB, 6, 1)
+        fetch(H_SLAB, 5, 1)
         fetch(1, 5, 1)
-        fetch(H_SLAB, 7, 1)
+        fetch(H_SLAB, 6, 1)
         fetch(1, 6, 1)
+        fetch(H_SLAB, 7, 1)
         fetch(1, 7, 1)
-        fetch(2, 0, 2)
+        fetch(2, 0, 1)
+        fetch(2, 1, 1)
         fetch(2, 2, 2)
         fetch(2, 4, 4)
 
@@ -219,15 +220,15 @@ def tile_hypernetfullyconnectedflexilayersizearch_pa_k_kernel(
         v1_sums = const.tile([P, V1_ROWS], F32)
         factor[V1_SLAB] = const.tile([P, V1_ROWS], F32, name="v1_factor")[:]
 
-        def pair_squares(s, pair):
-            bank = 2 * pair
+        def late_squares(s, bank, n):
             if s == V1_SLAB:
-                for b in (bank, bank + 1):
+                for b in range(bank, bank + n):
                     square(s, b, 1, v1_sums[:, b : b + 1])
                 return
-            if pair == 0:
-                sums[s] = stats.tile([P, SLAB_BANKS], F32, name="sums")[:, 0 : SLAB_BANKS // 2]
-            square(s, bank, 2, sums[s][:, pair : pair + 1])
+            if bank == 0:
+                sums[s] = stats.tile([P, SLAB_BANKS], F32, name="sums")[:, 0 : len(LATE_PIECES)]
+            piece = LATE_PIECES.index((bank, n))
+            square(s, bank, n, sums[s][:, piece : piece + 1])
 
         def v1_factors(first):
             cols = slice(first, first + 4)
@@ -242,7 +243,7 @@ def tile_hypernetfullyconnectedflexilayersizearch_pa_k_kernel(
 
         def prepare(s):
             if s == 2:
-                v0_squares(s, (2, 2, 4))
+                v0_squares(s, (1, 1, 2, 4))
                 return
             if s == GRAM_SLAB:
                 sums[s] = gram_sums[:, 0:1]
@@ -310,20 +311,23 @@ def tile_hypernetfullyconnectedflexilayersizearch_pa_k_kernel(
 
         def pool_squares(step):
             nc.gpsimd.tensor_copy(out=awaited[:], in_=last_codes[0])
-            values = slab_tile[POOL_SLAB][:, step * POOL_PIECE : (step + 1) * POOL_PIECE]
-            powers_tile = powers.tile([P, POOL_PIECE], F32, name="powers")
-            nc.gpsimd.tensor_tensor(out=powers_tile[:], in0=values, in1=values, op=ALU.mult)
+            start, width = sum(POOL_BLOCKS[:step]) * P, POOL_BLOCKS[step] * P
+            values = slab_tile[POOL_SLAB][:, start : start + width]
+            powers_tile = powers.tile([P, max(POOL_BLOCKS) * P], F32, name="powers")
+            nc.gpsimd.tensor_tensor(
+                out=powers_tile[:, 0:width], in0=values, in1=values, op=ALU.mult
+            )
             return powers_tile
 
         def pool_add(step, powers_tile):
-            for i in range(POOL_PIECE // P):
+            for i in range(POOL_BLOCKS[step]):
                 nc.tensor.matmul(
                     pool_acc[0][:, 0, :],
                     lhsT=powers_tile[:, i * P : (i + 1) * P],
                     rhs=ident[:],
                     is_transpose=True,
                     start=(step == 0 and i == 0),
-                    stop=(step == len(POOL_UNITS) - 1 and i == POOL_PIECE // P - 1),
+                    stop=(step == len(POOL_UNITS) - 1 and i == POOL_BLOCKS[step] - 1),
                 )
 
         def pool_total():
@@ -485,7 +489,8 @@ def tile_hypernetfullyconnectedflexilayersizearch_pa_k_kernel(
         transposes(0)
         scaled = 0
         gram = []
-        pairs = [(s, pair) for s in range(V0_SLABS, SLABS) for pair in range(SLAB_BANKS // 2)]
+        late = [(V0_SLABS, b, n) for b, n in LATE_PIECES]
+        late += [(V1_SLAB, b, 2) for b in range(0, SLAB_BANKS, 2)]
         for m, (s, first, n) in enumerate(UNITS):
             if m in POOL_UNITS:
                 need_factors(m + 1)
@@ -525,9 +530,8 @@ def tile_hypernetfullyconnectedflexilayersizearch_pa_k_kernel(
                 prepare(POOL_SLAB)
             if first == 0 and POOL_SLAB < s + 4 <= V1_SLAB:
                 prepare(s + 4)
-            due = SQUARES_FIRST + m - SHARE_FROM + 1 if m >= SHARE_FROM - 1 else 0
-            while pairs and len(pairs) > 8 - due:
-                pair_squares(*pairs.pop(0))
+            if m >= SHARE_FROM - 1 and late:
+                late_squares(*late.pop(0))
             if m == V1_FIRST:
                 group_hidden(0)
             if bank == 0:

from contextlib import ExitStack

import concourse.mybir as mybir
from concourse.masks import make_identity

BF16 = mybir.dt.bfloat16
F32 = mybir.dt.float32
U32 = mybir.dt.uint32
U8 = mybir.dt.uint8
FP8X4 = mybir.dt.float8_e4m3fn_x4
ALU = mybir.AluOpType
ACT = mybir.ActivationFunctionType

P = 128
D_IN = 8192
HIDDEN = 1024
K_PASS = 512
BANK = 512
PSUM_BANKS = 8

SLAB = 8192
BANK_VALUES = 2 * BANK
SLAB_BANKS = SLAB // BANK_VALUES
SLAB_PASSES = SLAB // K_PASS
BANK_PASSES = SLAB_PASSES // SLAB_BANKS
BANK_BLOCKS = BANK // P
H_SLAB = 0
V0_SLABS = HIDDEN // P
V1_SLAB = V0_SLABS + 1
SLABS = V1_SLAB + 1
V1_ROWS = SLAB // HIDDEN
L1_PASSES = HIDDEN // K_PASS
LEAD = 2
HALF_SLAB = ((0, 4), (4, 4))
QUARTERS = ((0, 2), (2, 2), (4, 2), (6, 2))
UNITS = (
    [(H_SLAB, b, n) for b, n in QUARTERS]
    + [(s, b, n) for s in range(1, V1_SLAB) for b, n in HALF_SLAB]
    + [(V1_SLAB, 0, 4), (V1_SLAB, 4, 2), (V1_SLAB, 6, 2)]
)
V1_FIRST = UNITS.index((V1_SLAB, 0, 4))
LAST = len(UNITS) - 1
GRAM_SLAB = 6
GRAM_BANKS = SLAB_BANKS - 1
GRAM_FROM = UNITS.index((1, 0, 4))
POOL_SLAB = 7
POOL_BLOCKS = (6, 4, 6, 4, 6, 4)
POOL_UNITS = [UNITS.index((s, b, 4)) for s, b in ((2, 0), (2, 4), (3, 0), (3, 4), (4, 0), (4, 4))]
POOL_VALUES = sum(POOL_BLOCKS) * P
POOL_DONE = POOL_UNITS[-1] + 1
EARLY_FETCHES = {
    3: ((GRAM_SLAB, 2, 2), (POOL_SLAB, 0, 2)),
    4: ((GRAM_SLAB, 4, 2),),
    5: ((POOL_SLAB, 2, 2), (GRAM_SLAB, 6, 2), (POOL_SLAB, 4, 4)),
}
UNREAD = max(SLAB // 2, SLAB - POOL_VALUES)
SHARE_FROM = UNITS.index((5, 0, 4))
SHARE = 2
LATE_PIECES = ((0, 4), (4, 2), (6, 2))

FLOPS = 2 * P * D_IN * HIDDEN + 2 * P * HIDDEN * HIDDEN


def tile_hypernetfullyconnectedflexilayersizearch_pa_k_kernel(
    tc, pooled_sum, count, V0, g0, b0, V1, g1, b1, out
):
    nc = tc.nc
    with ExitStack() as ctx:
        const = ctx.enter_context(tc.tile_pool(name="const", bufs=1))
        slabs = ctx.enter_context(tc.tile_pool(name="slabs", bufs=6))
        scratch = ctx.enter_context(tc.tile_pool(name="scratch", bufs=2))
        unread = ctx.enter_context(tc.tile_pool(name="unread", bufs=2))
        stats = ctx.enter_context(tc.tile_pool(name="stats", bufs=4))
        regroup = ctx.enter_context(tc.tile_pool(name="regroup", bufs=3))
        weights = ctx.enter_context(tc.tile_pool(name="weights", bufs=2))
        final = ctx.enter_context(tc.tile_pool(name="final", bufs=3))
        psum = ctx.enter_context(tc.psum_pool(name="psum", bufs=1))
        powers = ctx.enter_context(tc.tile_pool(name="powers", bufs=2))
        ctx.enter_context(tc.manual_schedule())
        v0_rows = V0.rearrange("(i2 p e) (a w) -> i2 e p a w", p=P, e=2, a=4)
        dram_rows = {H_SLAB: pooled_sum.rearrange("c (a w) -> c a w", a=4)}
        for i in range(V0_SLABS):
            dram_rows[1 + i] = v0_rows[i // 2, i % 2]
        dram_rows[V1_SLAB] = V1.rearrange("(a p e) k -> p a (e k)", p=P, e=2)

        slab_tile = {}
        sums = {}
        factor = {}
        codes = {}
        planes = {}
        raw = {}
        banks = {}
        grouped = {}
        awaited = const.tile([P, 1], BF16)
        last_codes = [None]
        pool_acc = []
        product = {}

        ring = list(range(PSUM_BANKS))
        held = {}

        def bank_tile(number):
            return psum.tile([P, BANK_BLOCKS, P], F32, tag="bank%d" % number, name="bank")

        def next_bank():
            ring.append(ring.pop(0))
            return bank_tile(ring[-1])

        def hold_bank(user):
            held[user] = ring.pop(0)
            return bank_tile(held[user])

        def put_back(user):
            ring.append(held[user])

        def new_slab(s):
            slab_tile[s] = slabs.tile([P, SLAB], BF16, name="slab")

        def fetch(s, bank, n):
            quarter, rest = divmod(bank, 2)
            if n == 1:
                src = dram_rows[s][:, quarter, rest * BANK_VALUES : (rest + 1) * BANK_VALUES]
                dst = slab_tile[s][:, bank * BANK_VALUES : (bank + 1) * BANK_VALUES]
            else:
                src = dram_rows[s][:, quarter : quarter + n // 2, :]
                dst = slab_tile[s][:, bank * BANK_VALUES : (bank + n) * BANK_VALUES].rearrange(
                    "p (a w) -> p a w", a=n // 2
                )
            nc.sync.dma_start(out=dst, in_=src)

        minus_half = const.tile([P, V1_ROWS], F32)
        nc.vector.memset(minus_half[:], -0.5)
        cnt = const.tile([P, 1], BF16)
        nc.scalar.dma_start(out=cnt[:], in_=count)
        table_load = const.tile([P, 1], F32)
        nc.scalar.activation(out=table_load[:], in_=minus_half[:, 0:1], func=ACT.Silu)
        vec_rows = const.tile([P, P], F32)
        nc.vector.memset(vec_rows[:], 0.0)
        for n, vec in enumerate((g0, b0, g1)):
            nc.scalar.dma_start(
                out=vec_rows[:].bitcast(BF16)[4 * n : 4 * n + 4, :],
                in_=vec.rearrange("(r w) -> r w", r=4),
            )

        for s in (H_SLAB, 1, 2):
            new_slab(s)

        fetch(H_SLAB, 0, 1)
        fetch(1, 0, 1)
        fetch(H_SLAB, 1, 1)
        fetch(1, 1, 1)
        fetch(H_SLAB, 2, 1)
        fetch(1, 2, 1)
        fetch(H_SLAB, 3, 1)
        fetch(1, 3, 1)
        fetch(H_SLAB, 4, 1)
        fetch(1, 4, 1)
        fetch(H_SLAB, 5, 1)
        fetch(1, 5, 1)
        fetch(H_SLAB, 6, 1)
        fetch(1, 6, 1)
        fetch(H_SLAB, 7, 1)
        fetch(1, 7, 1)
        fetch(2, 0, 1)
        fetch(2, 1, 1)
        fetch(2, 2, 2)
        fetch(2, 4, 4)

        ident = const.tile([P, P], F32)
        make_identity(nc, ident[:])

        vecs = const.tile([P, 3 * V0_SLABS], F32)
        bias0 = vecs[:, V0_SLABS : 2 * V0_SLABS]
        gain = {V1_SLAB: vecs[:, 2 * V0_SLABS : 3 * V0_SLABS]}
        for i in range(V0_SLABS):
            gain[1 + i] = vecs[:, i : i + 1]
        b1_all = const.tile([P, HIDDEN], BF16)

        per_count = const.tile([P, 1], F32)
        nc.vector.tensor_scalar_max(out=per_count[:], in0=cnt[:], scalar1=1.0)
        nc.vector.reciprocal(out=per_count[:], in_=per_count[:])
        factor[H_SLAB] = per_count[:]

        def square(s, bank, n, total):
            squares = unread.tile([P, UNREAD], BF16, name="squares")
            nc.scalar.activation(
                out=squares[:, 0 : n * BANK_VALUES],
                in_=slab_tile[s][:, bank * BANK_VALUES : (bank + n) * BANK_VALUES],
                func=ACT.Square,
                accum_out=total,
            )

        def one_over_length(result, lengths):
            width = result.shape[1]
            nc.gpsimd.tensor_tensor(
                out=result, in0=lengths, in1=minus_half[:, 0:width], op=ALU.pow
            )

        def v0_squares(s, pieces):
            sums[s] = stats.tile([P, SLAB_BANKS], F32, name="sums")[:, 0 : len(pieces)]
            bank = 0
            for i, n in enumerate(pieces):
                square(s, bank, n, sums[s][:, i : i + 1])
                bank += n

        def v0_factors(s):
            factor[s] = stats.tile([P, 1], F32, name="factor")[:]
            total = sums[s][:, 0:1]
            for i in range(1, sums[s].shape[1]):
                nc.gpsimd.tensor_tensor(
                    out=factor[s], in0=total, in1=sums[s][:, i : i + 1], op=ALU.add
                )
                total = factor[s]
            one_over_length(factor[s], total)

        gram_sums = const.tile([P, 2], F32)
        pool_sums = const.tile([P, 2], F32)
        ones = const.tile([P, 2], F32)
        nc.vector.memset(ones[:], 1.0)
        v1_sums = const.tile([P, V1_ROWS], F32)
        factor[V1_SLAB] = const.tile([P, V1_ROWS], F32, name="v1_factor")[:]

        def late_squares(s, bank, n):
            if s == V1_SLAB:
                for b in range(bank, bank + n):
                    square(s, b, 1, v1_sums[:, b : b + 1])
                return
            if bank == 0:
                sums[s] = stats.tile([P, SLAB_BANKS], F32, name="sums")[:, 0 : len(LATE_PIECES)]
            piece = LATE_PIECES.index((bank, n))
            square(s, bank, n, sums[s][:, piece : piece + 1])

        def v1_factors(first):
            cols = slice(first, first + 4)
            one_over_length(factor[V1_SLAB][:, cols], v1_sums[:, cols])

        def need_factors(m):
            s, first, n = UNITS[m]
            if s not in factor:
                v0_factors(s)
            if s == V1_SLAB and first % 4 == 0:
                v1_factors(first)

        def prepare(s):
            if s == 2:
                v0_squares(s, (1, 1, 2, 4))
                return
            if s == GRAM_SLAB:
                sums[s] = gram_sums[:, 0:1]
                square(s, GRAM_BANKS, SLAB_BANKS - GRAM_BANKS, gram_sums[:, 1:2])
                return
            if s == POOL_SLAB:
                sums[s] = pool_sums[:, 0:1]
                squares = unread.tile([P, UNREAD], BF16, name="squares")
                nc.scalar.activation(
                    out=squares[:, 0 : SLAB - POOL_VALUES],
                    in_=slab_tile[s][:, POOL_VALUES:SLAB],
                    func=ACT.Square,
                    accum_out=pool_sums[:, 1:2],
                )
                return
            new_slab(s)
            if s == 3:
                for early in (GRAM_SLAB, POOL_SLAB):
                    new_slab(early)
                fetch(GRAM_SLAB, 0, 2)
            for bank in range(0, SLAB_BANKS, 4):
                fetch(s, bank, 4)
            for early, bank, n in EARLY_FETCHES.get(s, ()):
                fetch(early, bank, n)
            if s == V1_SLAB:
                nc.sync.dma_start(out=b1_all[:], in_=b1.partition_broadcast(P))
            elif s < GRAM_SLAB:
                v0_squares(s, (4, 4))

        def scale(m):
            need_factors(m)
            s, b, n = UNITS[m]
            end = (b + n) * BANK_VALUES
            span = SLAB // factor[s].shape[1]
            piece = BANK_VALUES if s == H_SLAB else min(span, end - b * BANK_VALUES)
            for start in range(b * BANK_VALUES, end, piece):
                values = slab_tile[s][:, start : start + piece]
                row = slice(start // span, start // span + 1)
                if s == H_SLAB:
                    nc.vector.tensor_scalar_mul(
                        out=values, in0=values, scalar1=factor[s][:, row]
                    )
                else:
                    nc.vector.tensor_scalar(
                        out=values,
                        in0=values,
                        scalar1=factor[s][:, row],
                        scalar2=gain[s][:, row],
                        op0=ALU.mult,
                        op1=ALU.mult,
                    )

        def transposes(m):
            s, first, n = UNITS[m]
            words = slab_tile[s][:].bitcast(F32)
            banks[m] = []
            for b in range(first, first + n):
                xt = next_bank()
                for i in range(BANK_BLOCKS):
                    block = BANK_BLOCKS * b + i
                    nc.tensor.transpose(
                        xt[:, i, :], words[:, block * P : (block + 1) * P], ident[:]
                    )
                banks[m].append(xt)

        def pool_squares(step):
            nc.gpsimd.tensor_copy(out=awaited[:], in_=last_codes[0])
            start, width = sum(POOL_BLOCKS[:step]) * P, POOL_BLOCKS[step] * P
            values = slab_tile[POOL_SLAB][:, start : start + width]
            powers_tile = powers.tile([P, max(POOL_BLOCKS) * P], F32, name="powers")
            nc.gpsimd.tensor_tensor(
                out=powers_tile[:, 0:width], in0=values, in1=values, op=ALU.mult
            )
            return powers_tile

        def pool_add(step, powers_tile):
            for i in range(POOL_BLOCKS[step]):
                nc.tensor.matmul(
                    pool_acc[0][:, 0, :],
                    lhsT=powers_tile[:, i * P : (i + 1) * P],
                    rhs=ident[:],
                    is_transpose=True,
                    start=(step == 0 and i == 0),
                    stop=(step == len(POOL_UNITS) - 1 and i == POOL_BLOCKS[step] - 1),
                )

        def pool_total():
            part = scratch.tile([P, P], F32, name="pool_part")
            nc.vector.tensor_copy(out=part[:], in_=pool_acc[0][:, 0, :])
            nc.tensor.matmul(
                pool_acc[0][:, 1, 0:2], lhsT=part[:], rhs=ones[:], start=True, stop=True
            )

        def gram_transposes(b):
            words = slab_tile[GRAM_SLAB][:].bitcast(F32)
            raw[b] = next_bank()
            for i in range(BANK_BLOCKS):
                block = BANK_BLOCKS * b + i
                nc.tensor.transpose(raw[b][:, i, :], words[:, block * P : (block + 1) * P], ident[:])

        def gram_copy(b):
            words = scratch.tile([P, BANK_BLOCKS * P], F32, name="raw_words")
            nc.vector.tensor_copy(out=words[:], in_=raw[b][:].rearrange("p i r -> p (i r)"))
            raw[b] = words

        def gram_multiply(b):
            pairs = raw[b][:].bitcast(BF16).rearrange("p (i r e) -> p i r e", r=P, e=2)
            for i in range(BANK_BLOCKS):
                for e in range(2):
                    values = pairs[:, i, :, e]
                    nc.tensor.matmul(
                        gram[0][:, 0, :],
                        lhsT=values,
                        rhs=values,
                        start=(b == 0 and i == 0 and e == 0),
                        stop=(b == GRAM_BANKS - 1 and i == BANK_BLOCKS - 1 and e == 1),
                    )

        def gram_diagonal():
            diagonal = scratch.tile([P, P], F32, name="diagonal")
            nc.vector.scalar_tensor_tensor(
                out=diagonal[:],
                in0=gram[0][:, 0, :],
                scalar=gram_sums[:, 1:2],
                in1=ident[:],
                op0=ALU.add,
                op1=ALU.mult,
                accum_out=gram_sums[:, 0:1],
            )

        def empty_banks(m):
            n = UNITS[m][2]
            grouped[m] = regroup.tile(
                [P, n * BANK_PASSES, P, 2], F32, tag="grouped", name="grouped", align_bytes=64
            )
            for b, xt in enumerate(banks[m]):
                target = grouped[m][:, BANK_PASSES * b : BANK_PASSES * (b + 1), :, :]
                planes_uv = xt[:].rearrange("p (n u) r -> p n r u", u=2)
                if m >= V1_FIRST or (m >= SHARE_FROM and b >= n - (3 if (m - SHARE_FROM) % 4 == 1 or m >= V1_FIRST - 2 else SHARE)):
                    nc.scalar.copy(out=target, in_=planes_uv)
                else:
                    nc.vector.tensor_copy(out=target, in_=planes_uv)

        def quantise(m):
            s, first, n = UNITS[m]
            if first == 0:
                pool = weights if 1 <= s <= V0_SLABS else const
                label = "w0" if 1 <= s <= V0_SLABS else "slab%d" % s
                codes[s] = pool.tile(
                    [P, SLAB_PASSES, P], U32, name=label + "_codes", align_bytes=64
                )
                planes[s] = pool.tile(
                    [P, SLAB_PASSES, P], U8, name=label + "_planes", align_bytes=64
                )
            step = 1 if m == LAST else n
            for b in range(0, n, step):
                passes = slice(BANK_PASSES * (first + b), BANK_PASSES * (first + b + step))
                words = grouped[m][:, BANK_PASSES * b : BANK_PASSES * (b + step), :, :]
                last_codes[0] = codes[s][:, passes, :].rearrange("p n r -> p (n r)").bitcast(BF16)[
                    :, 0:1
                ]
                nc.vector.quantize_mx(
                    out=codes[s][:, passes, :].rearrange("p n r -> p (n r)").bitcast(FP8X4),
                    scales=planes[s][:, passes, :].rearrange("p n r -> p (n r)"),
                    in_=words.rearrange("p n r u -> p (n r u)").bitcast(BF16),
                )

        a0_rows = const.tile([P, V0_SLABS, P], BF16)
        a0_grouped = const.tile([P, L1_PASSES, P, 4], BF16, align_bytes=64)
        a0_codes = const.tile([P, L1_PASSES, P], U32, align_bytes=64)
        a0_planes = const.tile([P, L1_PASSES, P], U8, align_bytes=64)

        def multiply(m):
            s, first, banks_here = UNITS[m]
            if 1 <= s <= V0_SLABS:
                if first == 0 and (s - 1) % BANK_BLOCKS == 0:
                    acc = hold_bank(("products", s))
                    for q in range(BANK_BLOCKS):
                        product[s + q] = acc[:, q, :]
                for n in range(BANK_PASSES * first, BANK_PASSES * (first + banks_here)):
                    nc.tensor.matmul_mx(
                        out=product[s],
                        lhsT=codes[s][:, n, :].bitcast(FP8X4),
                        lhsT_scale=planes[s][:, n, :],
                        rhs=codes[H_SLAB][:, n, :].bitcast(FP8X4),
                        rhs_scale=planes[H_SLAB][:, n, :],
                        start=(n == 0),
                        stop=(n == SLAB_PASSES - 1),
                    )
            if s == V1_SLAB:
                product[m] = next_bank()[:].rearrange("p i r -> p (i r)")
                for i in range(first, first + banks_here):
                    cols = slice((i - first) * P, (i - first + 1) * P)
                    for n in range(L1_PASSES):
                        nc.tensor.matmul_mx(
                            out=product[m][:, cols],
                            lhsT=a0_codes[:, n, :].bitcast(FP8X4),
                            lhsT_scale=a0_planes[:, n, :],
                            rhs=codes[s][:, L1_PASSES * i + n, :].bitcast(FP8X4),
                            rhs_scale=planes[s][:, L1_PASSES * i + n, :],
                            start=(n == 0),
                            stop=(n == L1_PASSES - 1),
                        )

        def group_hidden(n):
            nc.vector.tensor_copy(
                out=a0_grouped[:, n, :, :],
                in_=a0_rows[:, 4 * n : 4 * n + 4, :].rearrange("p t c -> p c t"),
            )

        def quantise_hidden():
            nc.vector.quantize_mx(
                out=a0_codes[:].rearrange("p n c -> p (n c)").bitcast(FP8X4),
                scales=a0_planes[:].rearrange("p n c -> p (n c)"),
                in_=a0_grouped[:].rearrange("p n c t -> p (n c t)"),
            )

        def hidden_silu(s):
            i = s - 1
            nc.scalar.activation(
                out=a0_rows[:, i, :],
                in_=product[s],
                func=ACT.Silu,
                bias=bias0[:, i : i + 1],
            )

        def write_output(m):
            s, first, n = UNITS[m]
            width = n * P
            cols = slice(first * P, first * P + width)
            biased = final.tile([P, BANK], F32, name="biased")
            nc.vector.tensor_tensor(
                out=biased[:, 0:width].rearrange("c (i2 p e) -> c i2 p e", p=P, e=2),
                in0=product[m][:, 0:width].rearrange("c (i2 e p) -> c i2 p e", p=P, e=2),
                in1=b1_all[:, cols].rearrange("c (i2 p e) -> c i2 p e", p=P, e=2),
                op=ALU.add,
            )
            result = final.tile([P, BANK], F32, name="result")
            nc.scalar.activation(out=result[:, 0:width], in_=biased[:, 0:width], func=ACT.Silu)
            nc.sync.dma_start(out=out[:, cols], in_=result[:, 0:width])

        scale(0)
        transposes(0)
        scaled = 0
        gram = []
        late = [(V0_SLABS, b, n) for b, n in LATE_PIECES]
        late += [(V1_SLAB, b, 2) for b in range(0, SLAB_BANKS, 2)]
        for m, (s, first, n) in enumerate(UNITS):
            if m in POOL_UNITS:
                need_factors(m + 1)
                powers_tile = pool_squares(POOL_UNITS.index(m))
            empty_banks(m)
            if m == POOL_DONE + 1:
                pool_total()
            if m == POOL_DONE + 2:
                nc.vector.tensor_scalar_add(
                    out=pool_sums[:, 0:1], in0=pool_acc[0][:, 1, 0:1], scalar1=pool_sums[:, 1:2]
                )
                put_back("pool")
            bank = m - GRAM_FROM
            if 1 <= bank <= GRAM_BANKS:
                gram_copy(bank - 1)
            if bank == GRAM_BANKS + 1:
                gram_diagonal()
                put_back("gram")
            if m == 3:
                nc.vector.tensor_copy(out=vecs[:], in_=vec_t[:, 0, 0:12].bitcast(BF16))
            ahead = 2 if m + 2 >= V1_FIRST else 1
            while scaled < min(m + ahead, LAST):
                scaled += 1
                scale(scaled)
                transposes(scaled)
            if m == V1_FIRST:
                for done in range(1, V0_SLABS + 1):
                    hidden_silu(done)
            if m == 0:
                v0_squares(1, (1,) * SLAB_BANKS)
            if m == 2:
                vec_t = next_bank()
                nc.tensor.transpose(vec_t[:, 0, :], vec_rows[:], ident[:])
            if first == 0 and s + LEAD <= GRAM_SLAB:
                prepare(s + LEAD)
            if first == 0 and s + LEAD == GRAM_SLAB:
                prepare(POOL_SLAB)
            if first == 0 and POOL_SLAB < s + 4 <= V1_SLAB:
                prepare(s + 4)
            if m >= SHARE_FROM - 1 and late:
                late_squares(*late.pop(0))
            if m == V1_FIRST:
                group_hidden(0)
            if bank == 0:
                gram.append(hold_bank("gram"))
            if 0 <= bank < GRAM_BANKS:
                gram_transposes(bank)
            if 1 <= bank <= GRAM_BANKS:
                gram_multiply(bank - 1)
            quantise(m)
            if m == V1_FIRST:
                group_hidden(1)
                quantise_hidden()
            multiply(m)
            if m == POOL_UNITS[0]:
                pool_acc.append(hold_bank("pool"))
            if m in POOL_UNITS:
                pool_add(POOL_UNITS.index(m), powers_tile)
        for m in range(V1_FIRST, LAST + 1):
            write_output(m)
